import numpy as np
import ml_dtypes


def mxq(x, axis, fmt="e4m3"):
    dtype, down = {"e4m3": (ml_dtypes.float8_e4m3fn, 7), "e5m2": (ml_dtypes.float8_e5m2, 14)}[fmt]
    v = np.moveaxis(np.asarray(x, np.float32).astype(ml_dtypes.bfloat16).astype(np.float64), axis, -1)
    blocks = v.reshape(v.shape[:-1] + (-1, 32))
    amax = np.abs(blocks).max(-1, keepdims=True)
    byte = np.maximum(np.where(amax > 0, np.frexp(amax)[1] - 1 + 127, 0) - down, 1)
    scale = np.exp2(byte - 127.0)
    codes = (blocks / scale).astype(np.float32).astype(dtype).astype(np.float64)
    return np.moveaxis((codes * scale).reshape(v.shape), -1, axis)


WIDE = False


def mx_kscale(k):
    if not WIDE:
        return np.ones(k)
    levels = np.array([10, -10, 5, -5, 0])
    a = np.random.permutation(np.resize(levels, k // 512 * 4)).reshape(k // 512, 4)
    idx = np.arange(k)
    return np.exp2(a[idx // 512, idx % 128 // 32])


BF16 = ml_dtypes.bfloat16


def bf(x):
    return np.asarray(x, np.float32).astype(BF16)


def f64(x):
    return np.asarray(x).astype(np.float64)


B, HI, WI, D, HEADS, WIN = 1, 64, 64, 512, 4, 32
TOK = WIN * WIN
HD = D // HEADS
NW = (HI // WIN) * (WI // WIN)


def window_partition(x):
    return x.reshape(B, HI // WIN, WIN, WI // WIN, WIN, D).swapaxes(2, 3).reshape(B, NW, TOK, D)


def setup_inputs():
    s = mx_kscale(D)
    return {
        "x": bf(np.random.standard_normal((B, HI, WI, D)) * s),
        "q": bf(np.random.standard_normal((B, NW, HEADS, TOK, HD)) * 2.0),
        "k": bf(np.random.standard_normal((B, NW, HEADS, TOK, HD)) * 2.0),
        "wv": bf(np.random.standard_normal((D, D)) / np.sqrt(D) / s[:, None]),
        "bv": bf(np.random.standard_normal(D) * 0.2),
        "pos_bias": bf(np.random.standard_normal((HEADS, TOK, TOK))),
    }


def reference(x, q, k, wv, bv, pos_bias):
    win = window_partition(f64(x))
    v = (mxq(win, 3, "e4m3") @ mxq(f64(wv), 0, "e4m3")) + f64(bv)
    v = v.reshape(B * NW, TOK, HEADS, HD).swapaxes(-3, -2)
    qh = f64(q).reshape(B * NW, HEADS, TOK, HD)
    kh = f64(k).reshape(B * NW, HEADS, TOK, HD)
    logits = qh @ kh.swapaxes(2, 3) / np.sqrt(D)
    logits = logits + f64(pos_bias)
    logits = np.where(np.eye(TOK, dtype=bool), -np.inf, logits)
    e = np.exp(logits - logits.max(3, keepdims=True))
    out = (mxq(e, 3, "e4m3") @ mxq(v, 2, "e4m3")) / e.sum(3, keepdims=True)
    return out.swapaxes(-3, -2).reshape(B, NW, TOK, D)

@@ -1,0 +1,320 @@
+import math
+from contextlib import ExitStack
+
+import concourse.mybir as mybir
+from concourse.masks import make_identity
+
+BF16 = mybir.dt.bfloat16
+F32 = mybir.dt.float32
+U32 = mybir.dt.uint32
+U8 = mybir.dt.uint8
+FP8X4 = mybir.dt.float8_e4m3fn_x4
+ALU = mybir.AluOpType
+ACT = mybir.ActivationFunctionType
+
+P = 128
+PACK = 4
+WIN = 32
+GRID = 2
+NW = GRID * GRID
+HEADS = 4
+TOK = WIN * WIN
+D = 512
+HD = D // HEADS
+TILES = TOK // P
+PASSES = TOK // (P * PACK)
+BANK = 512
+HALVES = TOK // BANK
+QUAD = BANK // HD
+PAIRS = NW * HEADS
+SCALE = 1.0 / math.sqrt(D)
+MASKED = -1.0e30
+
+FLOPS = 2 * NW * TOK * D * D + 2 * (2 * PAIRS * TOK * TOK * HD)
+
+
+def tile_swintransformer_pa_kernel(tc, x, q, k, wv, bv, pos_bias, out):
+    nc = tc.nc
+    with ExitStack() as ctx:
+        const = ctx.enter_context(tc.tile_pool(name="const", bufs=1))
+        xin = ctx.enter_context(tc.tile_pool(name="xin", bufs=2))
+        proj = ctx.enter_context(tc.tile_pool(name="proj", bufs=1))
+        vkeep = ctx.enter_context(tc.tile_pool(name="vkeep", bufs=2))
+        qk = ctx.enter_context(tc.tile_pool(name="qk", bufs=2))
+        work = ctx.enter_context(tc.tile_pool(name="work", bufs=3))
+        stat = ctx.enter_context(tc.tile_pool(name="stat", bufs=6))
+        ps_lg = ctx.enter_context(tc.psum_pool(name="ps_lg", bufs=4))
+        ps_tr = ctx.enter_context(tc.psum_pool(name="ps_tr", bufs=2))
+        ps_o = ctx.enter_context(tc.psum_pool(name="ps_o", bufs=2))
+
+        ident_bf = const.tile([P, P], BF16, name="ident_bf")
+        make_identity(nc, ident_bf[:])
+        ident_f32 = const.tile([P, P], F32, name="ident_f32")
+        make_identity(nc, ident_f32[:])
+
+        raw = {}
+
+        def load_qk(m):
+            w, h = divmod(m, HEADS)
+            q_raw = qk.tile([P, TILES, HD], BF16, name="q_raw")
+            nc.sync.dma_start(out=q_raw[:], in_=q[0, w, h].rearrange("(i p) d -> p i d", p=P))
+            k_raw = qk.tile([P, TILES, HD], BF16, name="k_raw")
+            nc.sync.dma_start(out=k_raw[:], in_=k[0, w, h].rearrange("(i p) d -> p i d", p=P))
+            raw[m] = (q_raw, k_raw)
+
+        bias = [const.tile([P, TILES, TOK], BF16, name="bias%d" % h) for h in range(HEADS)]
+
+        def load_bias(h):
+            for i in range(TILES):
+                nc.sync.dma_start(out=bias[h][:, i, :], in_=pos_bias[h, i * P : (i + 1) * P, :])
+
+        def mask_bias(h, i):
+            block = bias[h][:, i, i * P : (i + 1) * P]
+            nc.gpsimd.affine_select(
+                out=block,
+                in_=block,
+                compare_op=ALU.not_equal,
+                fill=MASKED,
+                base=0,
+                pattern=[[-1, P]],
+                channel_multiplier=1,
+            )
+
+        x_raw = {}
+
+        def load_x(w):
+            wi, wj = divmod(w, GRID)
+            rows_per_tile = P // WIN
+            pixels = x[0, wi * WIN : (wi + 1) * WIN, wj * WIN : (wj + 1) * WIN, :]
+            by_row = pixels.rearrange("(j r) c d -> r c j d", r=rows_per_tile)
+            tile_x = xin.tile([P, TILES, D], BF16, name="x_raw")
+            for r in range(rows_per_tile):
+                nc.sync.dma_start(out=tile_x[r * WIN : (r + 1) * WIN, :, :], in_=by_row[r])
+            x_raw[w] = tile_x
+
+        load_qk(0)
+        nc.sync.dma_start(out=bias[0][:, 0, :], in_=pos_bias[0, 0:P, :])
+        w_raw = const.tile([P, PACK, D], BF16, name="w_raw")
+        nc.sync.dma_start(
+            out=w_raw[:].rearrange("p (u e) n -> p u (e n)", e=2),
+            in_=wv.rearrange("(u p e) n -> p u (e n)", u=2, e=2),
+        )
+        load_x(0)
+        bv_sb = const.tile([P, D], BF16, name="bv_sb")
+        nc.sync.dma_start(out=bv_sb[:], in_=bv.partition_broadcast(P))
+        for i in range(1, TILES):
+            nc.sync.dma_start(out=bias[0][:, i, :], in_=pos_bias[0, i * P : (i + 1) * P, :])
+        load_qk(1)
+        load_x(1)
+        load_bias(1)
+
+        w_grouped = const.tile([P, D, PACK], BF16, name="w_grouped", align_bytes=64)
+        nc.vector.tensor_copy(out=w_grouped[:], in_=w_raw[:].rearrange("p t n -> p n t"))
+        w_codes = const.tile([P, D], U32, name="w_codes", align_bytes=64)
+        w_scales = const.tile([P, D], U8, name="w_scales", align_bytes=64)
+        nc.vector.quantize_mx(
+            out=w_codes[:].bitcast(FP8X4),
+            scales=w_scales[:],
+            in_=w_grouped[:].rearrange("p n t -> p (n t)"),
+        )
+
+        qkT = {}
+
+        def transpose_qk(m):
+            turned = []
+            for source, label in zip(raw.pop(m), ("qT", "kT")):
+                turned_ps = ps_tr.tile([P, TILES, P], BF16, name="turned_ps", tag="tr")
+                for i in range(TILES):
+                    nc.tensor.transpose(out=turned_ps[:, i, :], in_=source[:, i, :], identity=ident_bf[:])
+                turned_sb = qk.tile([P, TILES, P], BF16, name=label)
+                nc.scalar.copy(out=turned_sb[:], in_=turned_ps[:])
+                turned.append(turned_sb)
+            qkT[m] = turned
+
+        px = {}
+        values = {}
+
+        def turn_x(w, j):
+            if j == 0:
+                px["grouped"] = proj.tile([P, TILES, P, PACK], BF16, name="x_grouped", align_bytes=64)
+            xT_ps = ps_lg.tile([P, 2, 2, P], F32, name="xT_ps", tag="lg")
+            for jj in range(2):
+                words = x_raw[w][:, j + jj, :].bitcast(F32)
+                for u in range(2):
+                    nc.tensor.transpose(
+                        out=xT_ps[:, jj, u, :], in_=words[:, u * P : (u + 1) * P], identity=ident_f32[:]
+                    )
+            nc.scalar.copy(
+                out=px["grouped"][:].bitcast(F32)[:, j : j + 2, :, :],
+                in_=xT_ps[:].rearrange("p j u k -> p j k u"),
+            )
+
+        def quantise_x(w):
+            x_raw.pop(w)
+            px["codes"] = proj.tile([P, TOK], U32, name="x_codes", align_bytes=64)
+            px["scales"] = proj.tile([P, TOK], U8, name="x_scales", align_bytes=64)
+            nc.vector.quantize_mx(
+                out=px["codes"][:].bitcast(FP8X4),
+                scales=px["scales"][:],
+                in_=px["grouped"][:].rearrange("p j k t -> p (j k t)"),
+            )
+            px["v_f32"] = proj.tile([P, TILES, D], F32, name="v_f32")
+
+        def project(w, j):
+            v_ps = ps_lg.tile([P, D], F32, name="v_ps", tag="lg")
+            tokens = slice(j * P, (j + 1) * P)
+            nc.tensor.matmul_mx(
+                out=v_ps[:],
+                lhsT=px["codes"][:, tokens].bitcast(FP8X4),
+                lhsT_scale=px["scales"][:, tokens],
+                rhs=w_codes[:].bitcast(FP8X4),
+                rhs_scale=w_scales[:],
+                start=True,
+                stop=True,
+            )
+            nc.scalar.copy(out=px["v_f32"][:, j, :], in_=v_ps[:])
+
+        def add_bv(w, piece):
+            if piece == 0:
+                px["v_grouped"] = proj.tile([P, PASSES, D, PACK], BF16, name="v_grouped", align_bytes=64)
+            g, h = divmod(piece, HEADS)
+            cols = slice(h * HD, (h + 1) * HD)
+            nc.gpsimd.tensor_tensor(
+                out=px["v_grouped"][:, g, cols, :],
+                in0=px["v_f32"][:, g * PACK : (g + 1) * PACK, cols].rearrange("p t c -> p c t"),
+                in1=bv_sb[:, cols].unsqueeze(2).to_broadcast([P, HD, PACK]),
+                op=ALU.add,
+            )
+
+        def quantise_v(w):
+            v_codes = vkeep.tile([P, PASSES, D], U32, name="v_codes", align_bytes=64)
+            v_scales = vkeep.tile([P, PASSES, D], U8, name="v_scales", align_bytes=64)
+            nc.vector.quantize_mx(
+                out=v_codes[:].rearrange("p g c -> p (g c)").bitcast(FP8X4),
+                scales=v_scales[:].rearrange("p g c -> p (g c)"),
+                in_=px["v_grouped"][:].rearrange("p g c t -> p (g c t)"),
+            )
+            values[w] = (v_codes, v_scales)
+
+        quad = {}
+
+        def attend(w, h, i):
+            qT, kT = qkT[w * HEADS + h]
+            v_codes, v_scales = values[w]
+            r = i % QUAD
+            if r == 0:
+                quad["rowsum"] = stat.tile([P, QUAD], F32, name="rowsum")
+                quad["o_ps"] = ps_o.tile([P, QUAD, HD], F32, name="o_ps")
+
+            logits = work.tile([P, TOK], F32, name="logits")
+            for c in range(HALVES):
+                keys = slice(c * BANK, (c + 1) * BANK)
+                qk_ps = ps_lg.tile([P, BANK], F32, name="qk_ps", tag="lg")
+                nc.tensor.matmul(out=qk_ps[:], lhsT=qT[:, i, :], rhs=kT[:].rearrange("d j p -> d (j p)")[:, keys], start=True, stop=True)
+                nc.vector.scalar_tensor_tensor(
+                    out=logits[:, keys],
+                    in0=qk_ps[:],
+                    scalar=SCALE,
+                    in1=bias[h][:, i, keys],
+                    op0=ALU.mult,
+                    op1=ALU.add,
+                )
+            neg_max = stat.tile([P, 1], F32, name="neg_max")
+            nc.vector.tensor_reduce(
+                out=neg_max[:], in_=logits[:], axis=mybir.AxisListType.X, op=ALU.max, negate=True
+            )
+            e = work.tile([P, TOK], BF16, name="e")
+            nc.scalar.activation(
+                out=e[:],
+                in_=logits[:],
+                func=ACT.Exp,
+                bias=neg_max[:],
+                scale=1.0,
+                accum_out=quad["rowsum"][:, r : r + 1],
+            )
+
+            eT_ps = ps_tr.tile([P, TILES, P], BF16, name="eT_ps", tag="tr")
+            for j in range(TILES):
+                nc.tensor.transpose(out=eT_ps[:, j, :], in_=e[:, j * P : (j + 1) * P], identity=ident_bf[:])
+            eT = work.tile([P, TILES, P], BF16, name="eT")
+            nc.scalar.copy(out=eT[:], in_=eT_ps[:])
+            e_grouped = work.tile([P, PASSES, P, PACK], BF16, name="e_grouped", align_bytes=64)
+            nc.gpsimd.tensor_scalar(
+                out=e_grouped[:],
+                in0=eT[:].rearrange("p (g t) n -> p g n t", t=PACK),
+                scalar1=1.0,
+                scalar2=0.0,
+                op0=ALU.mult,
+                op1=ALU.add,
+            )
+            e_codes = work.tile([P, PASSES * P], U32, name="e_codes", align_bytes=64)
+            e_scales = work.tile([P, PASSES * P], U8, name="e_scales", align_bytes=64)
+            nc.vector.quantize_mx(
+                out=e_codes[:].bitcast(FP8X4),
+                scales=e_scales[:],
+                in_=e_grouped[:].rearrange("p g n t -> p (g n t)"),
+            )
+            cols = slice(h * HD, (h + 1) * HD)
+            for g in range(PASSES):
+                queries = slice(g * P, (g + 1) * P)
+                nc.tensor.matmul_mx(
+                    out=quad["o_ps"][:, r, :],
+                    lhsT=e_codes[:, queries].bitcast(FP8X4),
+                    lhsT_scale=e_scales[:, queries],
+                    rhs=v_codes[:, g, cols].bitcast(FP8X4),
+                    rhs_scale=v_scales[:, g, cols],
+                    start=(g == 0),
+                    stop=(g == PASSES - 1),
+                )
+
+            if r == QUAD - 1:
+                recip = stat.tile([P, QUAD], F32, name="recip")
+                nc.vector.reciprocal(out=recip[:], in_=quad["rowsum"][:])
+                o_sb = work.tile([P, QUAD, HD], F32, name="o_sb")
+                for rr in range(QUAD):
+                    nc.scalar.activation(
+                        out=o_sb[:, rr, :], in_=quad["o_ps"][:, rr, :], func=ACT.Copy, scale=recip[:, rr : rr + 1]
+                    )
+                nc.scalar.dma_start(
+                    out=out[0, w].rearrange("(i p) c -> p i c", p=P)[:, i - r : i + 1, cols], in_=o_sb[:]
+                )
+
+        for i in range(TILES):
+            mask_bias(0, i)
+        transpose_qk(0)
+        for j in range(0, TILES, 2):
+            turn_x(0, j)
+        quantise_x(0)
+        for j in range(TILES):
+            project(0, j)
+        for piece in range(TILES):
+            add_bv(0, piece)
+        quantise_v(0)
+
+        for w in range(NW):
+            for h in range(HEADS):
+                m = w * HEADS + h
+                for i in range(TILES):
+                    attend(w, h, i)
+                    if i == 0 and m + 2 < PAIRS:
+                        load_qk(m + 2)
+                    if i == 3 and m + 1 < PAIRS:
+                        transpose_qk(m + 1)
+                    if w == 0 and i == 0 and h + 2 < HEADS:
+                        load_bias(h + 2)
+                    if w == 0 and h + 1 < HEADS:
+                        mask_bias(h + 1, i)
+                    if w + 1 < NW:
+                        if h == 0 and i % 2 == 0:
+                            turn_x(w + 1, i)
+                        if h == 1 and i == 0:
+                            quantise_x(w + 1)
+                        if h == 1:
+                            project(w + 1, i)
+                        if h == 2:
+                            add_bv(w + 1, i)
+                        if h == 3 and i == 0:
+                            quantise_v(w + 1)
+                    if h == 3 and i == 0 and w + 2 < NW:
+                        load_x(w + 2)
+                qkT.pop(m)

@@ -27,6 +27,8 @@ BANK = 512
 HALVES = TOK // BANK
 QUAD = BANK // HD
 PAIRS = NW * HEADS
+N_TILES = PAIRS * TILES
+LAG = QUAD
 SCALE = 1.0 / math.sqrt(D)
 MASKED = -1.0e30
 
@@ -42,6 +44,7 @@ def tile_swintransformer_pa_kernel(tc, x, q, k, wv, bv, pos_bias, out):
         vkeep = ctx.enter_context(tc.tile_pool(name="vkeep", bufs=2))
         qk = ctx.enter_context(tc.tile_pool(name="qk", bufs=2))
         work = ctx.enter_context(tc.tile_pool(name="work", bufs=3))
+        packed = ctx.enter_context(tc.tile_pool(name="packed", bufs=8))
         stat = ctx.enter_context(tc.tile_pool(name="stat", bufs=6))
         ps_lg = ctx.enter_context(tc.psum_pool(name="ps_lg", bufs=4))
         ps_tr = ctx.enter_context(tc.psum_pool(name="ps_tr", bufs=2))
@@ -196,21 +199,29 @@ def tile_swintransformer_pa_kernel(tc, x, q, k, wv, bv, pos_bias, out):
             )
             values[w] = (v_codes, v_scales)
 
-        quad = {}
+        sums = {}
+        weights = {}
+        o_rows = {}
 
-        def attend(w, h, i):
-            qT, kT = qkT[w * HEADS + h]
-            v_codes, v_scales = values[w]
-            r = i % QUAD
+        def softmax_tile(n):
+            m, i = divmod(n, TILES)
+            h = m % HEADS
+            qT, kT = qkT[m]
+            group, r = divmod(n, QUAD)
             if r == 0:
-                quad["rowsum"] = stat.tile([P, QUAD], F32, name="rowsum")
-                quad["o_ps"] = ps_o.tile([P, QUAD, HD], F32, name="o_ps")
+                sums[group] = stat.tile([P, QUAD], F32, name="rowsum")
 
             logits = work.tile([P, TOK], F32, name="logits")
             for c in range(HALVES):
                 keys = slice(c * BANK, (c + 1) * BANK)
                 qk_ps = ps_lg.tile([P, BANK], F32, name="qk_ps", tag="lg")
-                nc.tensor.matmul(out=qk_ps[:], lhsT=qT[:, i, :], rhs=kT[:].rearrange("d j p -> d (j p)")[:, keys], start=True, stop=True)
+                nc.tensor.matmul(
+                    out=qk_ps[:],
+                    lhsT=qT[:, i, :],
+                    rhs=kT[:].rearrange("d j p -> d (j p)")[:, keys],
+                    start=True,
+                    stop=True,
+                )
                 nc.vector.scalar_tensor_tensor(
                     out=logits[:, keys],
                     in0=qk_ps[:],
@@ -230,7 +241,7 @@ def tile_swintransformer_pa_kernel(tc, x, q, k, wv, bv, pos_bias, out):
                 func=ACT.Exp,
                 bias=neg_max[:],
                 scale=1.0,
-                accum_out=quad["rowsum"][:, r : r + 1],
+                accum_out=sums[group][:, r : r + 1],
             )
 
             eT_ps = ps_tr.tile([P, TILES, P], BF16, name="eT_ps", tag="tr")
@@ -247,37 +258,49 @@ def tile_swintransformer_pa_kernel(tc, x, q, k, wv, bv, pos_bias, out):
                 op0=ALU.mult,
                 op1=ALU.add,
             )
-            e_codes = work.tile([P, PASSES * P], U32, name="e_codes", align_bytes=64)
-            e_scales = work.tile([P, PASSES * P], U8, name="e_scales", align_bytes=64)
+            e_codes = packed.tile([P, PASSES * P], U32, name="e_codes", align_bytes=64)
+            e_scales = packed.tile([P, PASSES * P], U8, name="e_scales", align_bytes=64)
             nc.vector.quantize_mx(
                 out=e_codes[:].bitcast(FP8X4),
                 scales=e_scales[:],
                 in_=e_grouped[:].rearrange("p g n t -> p (g n t)"),
             )
-            cols = slice(h * HD, (h + 1) * HD)
+            weights[n] = (e_codes, e_scales)
+            if r == QUAD - 1:
+                recip = stat.tile([P, QUAD], F32, name="recip")
+                nc.vector.reciprocal(out=recip[:], in_=sums[group][:])
+                sums[group] = recip
+
+        def finish_tile(n):
+            m, i = divmod(n, TILES)
+            w, h = divmod(m, HEADS)
+            group, r = divmod(n, QUAD)
+            v_codes, v_scales = values[w]
+            e_codes, e_scales = weights.pop(n)
+            o_ps = ps_o.tile([P, D], F32, name="o_ps")
             for g in range(PASSES):
                 queries = slice(g * P, (g + 1) * P)
                 nc.tensor.matmul_mx(
-                    out=quad["o_ps"][:, r, :],
+                    out=o_ps[:],
                     lhsT=e_codes[:, queries].bitcast(FP8X4),
                     lhsT_scale=e_scales[:, queries],
-                    rhs=v_codes[:, g, cols].bitcast(FP8X4),
-                    rhs_scale=v_scales[:, g, cols],
+                    rhs=v_codes[:, g, :].bitcast(FP8X4),
+                    rhs_scale=v_scales[:, g, :],
                     start=(g == 0),
                     stop=(g == PASSES - 1),
                 )
-
+            if r == 0:
+                o_rows[group] = work.tile([P, QUAD, HD], F32, name="o_sb")
+            cols = slice(h * HD, (h + 1) * HD)
+            nc.scalar.activation(
+                out=o_rows[group][:, r, :], in_=o_ps[:, cols], func=ACT.Copy, scale=sums[group][:, r : r + 1]
+            )
             if r == QUAD - 1:
-                recip = stat.tile([P, QUAD], F32, name="recip")
-                nc.vector.reciprocal(out=recip[:], in_=quad["rowsum"][:])
-                o_sb = work.tile([P, QUAD, HD], F32, name="o_sb")
-                for rr in range(QUAD):
-                    nc.scalar.activation(
-                        out=o_sb[:, rr, :], in_=quad["o_ps"][:, rr, :], func=ACT.Copy, scale=recip[:, rr : rr + 1]
-                    )
                 nc.scalar.dma_start(
-                    out=out[0, w].rearrange("(i p) c -> p i c", p=P)[:, i - r : i + 1, cols], in_=o_sb[:]
+                    out=out[0, w].rearrange("(i p) c -> p i c", p=P)[:, i - r : i + 1, cols],
+                    in_=o_rows.pop(group)[:],
                 )
+                sums.pop(group)
 
         for i in range(TILES):
             mask_bias(0, i)
@@ -291,30 +314,32 @@ def tile_swintransformer_pa_kernel(tc, x, q, k, wv, bv, pos_bias, out):
             add_bv(0, piece)
         quantise_v(0)
 
-        for w in range(NW):
-            for h in range(HEADS):
-                m = w * HEADS + h
-                for i in range(TILES):
-                    attend(w, h, i)
-                    if i == 0 and m + 2 < PAIRS:
-                        load_qk(m + 2)
-                    if i == 3 and m + 1 < PAIRS:
-                        transpose_qk(m + 1)
-                    if w == 0 and i == 0 and h + 2 < HEADS:
-                        load_bias(h + 2)
-                    if w == 0 and h + 1 < HEADS:
-                        mask_bias(h + 1, i)
-                    if w + 1 < NW:
-                        if h == 0 and i % 2 == 0:
-                            turn_x(w + 1, i)
-                        if h == 1 and i == 0:
-                            quantise_x(w + 1)
-                        if h == 1:
-                            project(w + 1, i)
-                        if h == 2:
-                            add_bv(w + 1, i)
-                        if h == 3 and i == 0:
-                            quantise_v(w + 1)
-                    if h == 3 and i == 0 and w + 2 < NW:
-                        load_x(w + 2)
-                qkT.pop(m)
+        for n in range(N_TILES + LAG):
+            if n >= LAG:
+                finish_tile(n - LAG)
+            if n >= N_TILES:
+                continue
+            softmax_tile(n)
+            m, i = divmod(n, TILES)
+            w, h = divmod(m, HEADS)
+            if i == 0 and m + 2 < PAIRS:
+                load_qk(m + 2)
+            if i == 3 and m + 1 < PAIRS:
+                transpose_qk(m + 1)
+            if w == 0 and i == 0 and h + 2 < HEADS:
+                load_bias(h + 2)
+            if w == 0 and h + 1 < HEADS:
+                mask_bias(h + 1, i)
+            if w + 1 < NW:
+                if h == 0 and i % 2 == 0:
+                    turn_x(w + 1, i)
+                if h == 1 and i == 0:
+                    quantise_x(w + 1)
+                if h == 1:
+                    project(w + 1, i)
+                if h == 2:
+                    add_bv(w + 1, i)
+                if h == 3 and i == 0:
+                    quantise_v(w + 1)
+            if h == 3 and i == 0 and w + 2 < NW:
+                load_x(w + 2)

@@ -28,7 +28,6 @@ HALVES = TOK // BANK
 QUAD = BANK // HD
 PAIRS = NW * HEADS
 N_TILES = PAIRS * TILES
-LAG = QUAD
 SCALE = 1.0 / math.sqrt(D)
 MASKED = -1.0e30
 
@@ -43,12 +42,12 @@ def tile_swintransformer_pa_kernel(tc, x, q, k, wv, bv, pos_bias, out):
         proj = ctx.enter_context(tc.tile_pool(name="proj", bufs=1))
         vkeep = ctx.enter_context(tc.tile_pool(name="vkeep", bufs=2))
         qk = ctx.enter_context(tc.tile_pool(name="qk", bufs=2))
-        work = ctx.enter_context(tc.tile_pool(name="work", bufs=3))
-        packed = ctx.enter_context(tc.tile_pool(name="packed", bufs=8))
+        work = ctx.enter_context(tc.tile_pool(name="work", bufs=4))
         stat = ctx.enter_context(tc.tile_pool(name="stat", bufs=6))
         ps_lg = ctx.enter_context(tc.psum_pool(name="ps_lg", bufs=4))
         ps_tr = ctx.enter_context(tc.psum_pool(name="ps_tr", bufs=2))
         ps_o = ctx.enter_context(tc.psum_pool(name="ps_o", bufs=2))
+        ctx.enter_context(tc.manual_schedule())
 
         ident_bf = const.tile([P, P], BF16, name="ident_bf")
         make_identity(nc, ident_bf[:])
@@ -63,7 +62,7 @@ def tile_swintransformer_pa_kernel(tc, x, q, k, wv, bv, pos_bias, out):
             nc.sync.dma_start(out=q_raw[:], in_=q[0, w, h].rearrange("(i p) d -> p i d", p=P))
             k_raw = qk.tile([P, TILES, HD], BF16, name="k_raw")
             nc.sync.dma_start(out=k_raw[:], in_=k[0, w, h].rearrange("(i p) d -> p i d", p=P))
-            raw[m] = (q_raw, k_raw)
+            raw[m] = {"q": q_raw, "k": k_raw}
 
         bias = [const.tile([P, TILES, TOK], BF16, name="bias%d" % h) for h in range(HEADS)]
 
@@ -95,21 +94,19 @@ def tile_swintransformer_pa_kernel(tc, x, q, k, wv, bv, pos_bias, out):
                 nc.sync.dma_start(out=tile_x[r * WIN : (r + 1) * WIN, :, :], in_=by_row[r])
             x_raw[w] = tile_x
 
-        load_qk(0)
-        nc.sync.dma_start(out=bias[0][:, 0, :], in_=pos_bias[0, 0:P, :])
+        load_x(0)
         w_raw = const.tile([P, PACK, D], BF16, name="w_raw")
         nc.sync.dma_start(
             out=w_raw[:].rearrange("p (u e) n -> p u (e n)", e=2),
             in_=wv.rearrange("(u p e) n -> p u (e n)", u=2, e=2),
         )
-        load_x(0)
+        load_qk(0)
+        load_bias(0)
         bv_sb = const.tile([P, D], BF16, name="bv_sb")
         nc.sync.dma_start(out=bv_sb[:], in_=bv.partition_broadcast(P))
-        for i in range(1, TILES):
-            nc.sync.dma_start(out=bias[0][:, i, :], in_=pos_bias[0, i * P : (i + 1) * P, :])
         load_qk(1)
-        load_x(1)
         load_bias(1)
+        load_x(1)
 
         w_grouped = const.tile([P, D, PACK], BF16, name="w_grouped", align_bytes=64)
         nc.vector.tensor_copy(out=w_grouped[:], in_=w_raw[:].rearrange("p t n -> p n t"))
@@ -121,18 +118,16 @@ def tile_swintransformer_pa_kernel(tc, x, q, k, wv, bv, pos_bias, out):
             in_=w_grouped[:].rearrange("p n t -> p (n t)"),
         )
 
-        qkT = {}
+        turned = {}
 
-        def transpose_qk(m):
-            turned = []
-            for source, label in zip(raw.pop(m), ("qT", "kT")):
-                turned_ps = ps_tr.tile([P, TILES, P], BF16, name="turned_ps", tag="tr")
-                for i in range(TILES):
-                    nc.tensor.transpose(out=turned_ps[:, i, :], in_=source[:, i, :], identity=ident_bf[:])
-                turned_sb = qk.tile([P, TILES, P], BF16, name=label)
-                nc.scalar.copy(out=turned_sb[:], in_=turned_ps[:])
-                turned.append(turned_sb)
-            qkT[m] = turned
+        def transpose_qk(m, which):
+            source = raw[m].pop(which)
+            turned_ps = ps_tr.tile([P, TILES, P], BF16, name="turned_ps", tag="tr")
+            for i in range(TILES):
+                nc.tensor.transpose(out=turned_ps[:, i, :], in_=source[:, i, :], identity=ident_bf[:])
+            turned_sb = qk.tile([P, TILES, P], BF16, name=which + "T")
+            nc.scalar.copy(out=turned_sb[:], in_=turned_ps[:])
+            turned[(m, which)] = turned_sb
 
         px = {}
         values = {}
@@ -199,89 +194,110 @@ def tile_swintransformer_pa_kernel(tc, x, q, k, wv, bv, pos_bias, out):
             )
             values[w] = (v_codes, v_scales)
 
+        qk_banks = {}
+        logits = {}
+        neg_max = {}
         sums = {}
+        e_rows = {}
+        eT_banks = {}
+        eT_planes = {}
+        e_groups = {}
         weights = {}
+        o_banks = {}
         o_rows = {}
 
-        def softmax_tile(n):
+        def multiply_qk(n):
             m, i = divmod(n, TILES)
-            h = m % HEADS
-            qT, kT = qkT[m]
-            group, r = divmod(n, QUAD)
-            if r == 0:
-                sums[group] = stat.tile([P, QUAD], F32, name="rowsum")
-
-            logits = work.tile([P, TOK], F32, name="logits")
+            qT, kT = turned[(m, "q")], turned[(m, "k")]
+            qk_banks[n] = []
             for c in range(HALVES):
-                keys = slice(c * BANK, (c + 1) * BANK)
                 qk_ps = ps_lg.tile([P, BANK], F32, name="qk_ps", tag="lg")
                 nc.tensor.matmul(
                     out=qk_ps[:],
                     lhsT=qT[:, i, :],
-                    rhs=kT[:].rearrange("d j p -> d (j p)")[:, keys],
+                    rhs=kT[:].rearrange("d j p -> d (j p)")[:, c * BANK : (c + 1) * BANK],
                     start=True,
                     stop=True,
                 )
+                qk_banks[n].append(qk_ps)
+
+        def add_bias_take_max(n):
+            m, i = divmod(n, TILES)
+            h = m % HEADS
+            logits[n] = work.tile([P, TOK], F32, name="logits")
+            for c, qk_ps in enumerate(qk_banks.pop(n)):
+                keys = slice(c * BANK, (c + 1) * BANK)
                 nc.vector.scalar_tensor_tensor(
-                    out=logits[:, keys],
+                    out=logits[n][:, keys],
                     in0=qk_ps[:],
                     scalar=SCALE,
                     in1=bias[h][:, i, keys],
                     op0=ALU.mult,
                     op1=ALU.add,
                 )
-            neg_max = stat.tile([P, 1], F32, name="neg_max")
+            neg_max[n] = stat.tile([P, 1], F32, name="neg_max")
             nc.vector.tensor_reduce(
-                out=neg_max[:], in_=logits[:], axis=mybir.AxisListType.X, op=ALU.max, negate=True
+                out=neg_max[n][:], in_=logits[n][:], axis=mybir.AxisListType.X, op=ALU.max, negate=True
             )
-            e = work.tile([P, TOK], BF16, name="e")
+
+        def exponentiate(n):
+            group, r = divmod(n, QUAD)
+            if r == 0:
+                sums[group] = stat.tile([P, QUAD], F32, name="rowsum")
+            e_rows[n] = work.tile([P, TOK], BF16, name="e")
             nc.scalar.activation(
-                out=e[:],
-                in_=logits[:],
+                out=e_rows[n][:],
+                in_=logits.pop(n)[:],
                 func=ACT.Exp,
-                bias=neg_max[:],
+                bias=neg_max.pop(n)[:],
                 scale=1.0,
                 accum_out=sums[group][:, r : r + 1],
             )
 
-            eT_ps = ps_tr.tile([P, TILES, P], BF16, name="eT_ps", tag="tr")
+        def invert_sums(group):
+            recip = stat.tile([P, QUAD], F32, name="recip")
+            nc.vector.reciprocal(out=recip[:], in_=sums[group][:])
+            sums[group] = recip
+
+        def turn_e(n):
+            e = e_rows.pop(n)
+            eT_banks[n] = ps_tr.tile([P, TILES, P], BF16, name="eT_ps", tag="tr")
             for j in range(TILES):
-                nc.tensor.transpose(out=eT_ps[:, j, :], in_=e[:, j * P : (j + 1) * P], identity=ident_bf[:])
-            eT = work.tile([P, TILES, P], BF16, name="eT")
-            nc.scalar.copy(out=eT[:], in_=eT_ps[:])
-            e_grouped = work.tile([P, PASSES, P, PACK], BF16, name="e_grouped", align_bytes=64)
+                nc.tensor.transpose(out=eT_banks[n][:, j, :], in_=e[:, j * P : (j + 1) * P], identity=ident_bf[:])
+
+        def copy_eT(n):
+            eT_planes[n] = work.tile([P, TILES, P], BF16, name="eT")
+            nc.scalar.copy(out=eT_planes[n][:], in_=eT_banks.pop(n)[:])
+
+        def regroup_e(n):
+            e_groups[n] = work.tile([P, PASSES, P, PACK], BF16, name="e_grouped", align_bytes=64)
             nc.gpsimd.tensor_scalar(
-                out=e_grouped[:],
-                in0=eT[:].rearrange("p (g t) n -> p g n t", t=PACK),
+                out=e_groups[n][:],
+                in0=eT_planes.pop(n)[:].rearrange("p (g t) n -> p g n t", t=PACK),
                 scalar1=1.0,
                 scalar2=0.0,
                 op0=ALU.mult,
                 op1=ALU.add,
             )
-            e_codes = packed.tile([P, PASSES * P], U32, name="e_codes", align_bytes=64)
-            e_scales = packed.tile([P, PASSES * P], U8, name="e_scales", align_bytes=64)
+
+        def quantise_e(n):
+            e_codes = work.tile([P, PASSES * P], U32, name="e_codes", align_bytes=64)
+            e_scales = work.tile([P, PASSES * P], U8, name="e_scales", align_bytes=64)
             nc.vector.quantize_mx(
                 out=e_codes[:].bitcast(FP8X4),
                 scales=e_scales[:],
-                in_=e_grouped[:].rearrange("p g n t -> p (g n t)"),
+                in_=e_groups.pop(n)[:].rearrange("p g n t -> p (g n t)"),
             )
             weights[n] = (e_codes, e_scales)
-            if r == QUAD - 1:
-                recip = stat.tile([P, QUAD], F32, name="recip")
-                nc.vector.reciprocal(out=recip[:], in_=sums[group][:])
-                sums[group] = recip
 
-        def finish_tile(n):
-            m, i = divmod(n, TILES)
-            w, h = divmod(m, HEADS)
-            group, r = divmod(n, QUAD)
-            v_codes, v_scales = values[w]
+        def multiply_v(n):
+            v_codes, v_scales = values[n // (HEADS * TILES)]
             e_codes, e_scales = weights.pop(n)
-            o_ps = ps_o.tile([P, D], F32, name="o_ps")
+            o_banks[n] = ps_o.tile([P, D], F32, name="o_ps")
             for g in range(PASSES):
                 queries = slice(g * P, (g + 1) * P)
                 nc.tensor.matmul_mx(
-                    out=o_ps[:],
+                    out=o_banks[n][:],
                     lhsT=e_codes[:, queries].bitcast(FP8X4),
                     lhsT_scale=e_scales[:, queries],
                     rhs=v_codes[:, g, :].bitcast(FP8X4),
@@ -289,57 +305,89 @@ def tile_swintransformer_pa_kernel(tc, x, q, k, wv, bv, pos_bias, out):
                     start=(g == 0),
                     stop=(g == PASSES - 1),
                 )
+
+        def scale_rows(n):
+            m, i = divmod(n, TILES)
+            w, h = divmod(m, HEADS)
+            group, r = divmod(n, QUAD)
             if r == 0:
                 o_rows[group] = work.tile([P, QUAD, HD], F32, name="o_sb")
             cols = slice(h * HD, (h + 1) * HD)
             nc.scalar.activation(
-                out=o_rows[group][:, r, :], in_=o_ps[:, cols], func=ACT.Copy, scale=sums[group][:, r : r + 1]
+                out=o_rows[group][:, r, :],
+                in_=o_banks.pop(n)[:, cols],
+                func=ACT.Copy,
+                scale=sums[group][:, r : r + 1],
             )
             if r == QUAD - 1:
-                nc.scalar.dma_start(
+                nc.sync.dma_start(
                     out=out[0, w].rearrange("(i p) c -> p i c", p=P)[:, i - r : i + 1, cols],
                     in_=o_rows.pop(group)[:],
                 )
                 sums.pop(group)
 
-        for i in range(TILES):
-            mask_bias(0, i)
-        transpose_qk(0)
-        for j in range(0, TILES, 2):
-            turn_x(0, j)
-        quantise_x(0)
-        for j in range(TILES):
-            project(0, j)
-        for piece in range(TILES):
-            add_bv(0, piece)
-        quantise_v(0)
-
-        for n in range(N_TILES + LAG):
-            if n >= LAG:
-                finish_tile(n - LAG)
-            if n >= N_TILES:
-                continue
-            softmax_tile(n)
+        def side_work(n):
             m, i = divmod(n, TILES)
             w, h = divmod(m, HEADS)
             if i == 0 and m + 2 < PAIRS:
                 load_qk(m + 2)
-            if i == 3 and m + 1 < PAIRS:
-                transpose_qk(m + 1)
+            if i == 2 and m + 1 < PAIRS:
+                transpose_qk(m + 1, "q")
+            if i == 4 and m + 1 < PAIRS:
+                transpose_qk(m + 1, "k")
             if w == 0 and i == 0 and h + 2 < HEADS:
                 load_bias(h + 2)
             if w == 0 and h + 1 < HEADS:
                 mask_bias(h + 1, i)
             if w + 1 < NW:
-                if h == 0 and i % 2 == 0:
-                    turn_x(w + 1, i)
+                if h == 0 and i >= TILES // 2:
+                    turn_x(w + 1, 2 * (i - TILES // 2))
                 if h == 1 and i == 0:
                     quantise_x(w + 1)
                 if h == 1:
                     project(w + 1, i)
                 if h == 2:
                     add_bv(w + 1, i)
-                if h == 3 and i == 0:
-                    quantise_v(w + 1)
             if h == 3 and i == 0 and w + 2 < NW:
                 load_x(w + 2)
+
+        for j in range(0, TILES, 2):
+            turn_x(0, j)
+        quantise_x(0)
+        transpose_qk(0, "q")
+        transpose_qk(0, "k")
+        multiply_qk(0)
+        for i in range(TILES):
+            mask_bias(0, i)
+        for j in range(TILES):
+            project(0, j)
+        for piece in range(TILES):
+            add_bv(0, piece)
+
+        def tile_exists(n):
+            return 0 <= n < N_TILES
+
+        for s in range(N_TILES + 7):
+            if tile_exists(s + 1):
+                multiply_qk(s + 1)
+            if tile_exists(s):
+                add_bias_take_max(s)
+            if tile_exists(s - 1):
+                exponentiate(s - 1)
+            if tile_exists(s - 2):
+                copy_eT(s - 2)
+                regroup_e(s - 2)
+            if tile_exists(s - 4):
+                if (s - 4) % (HEADS * TILES) == 0:
+                    quantise_v((s - 4) // (HEADS * TILES))
+                quantise_e(s - 4)
+            if tile_exists(s - 1) and (s - 1) % QUAD == QUAD - 1:
+                invert_sums((s - 1) // QUAD)
+            if tile_exists(s - 5):
+                multiply_v(s - 5)
+            if tile_exists(s - 6):
+                scale_rows(s - 6)
+            if tile_exists(s):
+                side_work(s)
+            if tile_exists(s - 1):
+                turn_e(s - 1)

@@ -221,7 +221,7 @@ def tile_swintransformer_pa_kernel(tc, x, q, k, wv, bv, pos_bias, out):
                 )
                 qk_banks[n].append(qk_ps)
 
-        def add_bias_take_max(n):
+        def add_bias(n):
             m, i = divmod(n, TILES)
             h = m % HEADS
             logits[n] = work.tile([P, TOK], F32, name="logits")
@@ -235,6 +235,8 @@ def tile_swintransformer_pa_kernel(tc, x, q, k, wv, bv, pos_bias, out):
                     op0=ALU.mult,
                     op1=ALU.add,
                 )
+
+        def take_max(n):
             neg_max[n] = stat.tile([P, 1], F32, name="neg_max")
             nc.vector.tensor_reduce(
                 out=neg_max[n][:], in_=logits[n][:], axis=mybir.AxisListType.X, op=ALU.max, negate=True
@@ -371,7 +373,7 @@ def tile_swintransformer_pa_kernel(tc, x, q, k, wv, bv, pos_bias, out):
             if tile_exists(s + 1):
                 multiply_qk(s + 1)
             if tile_exists(s):
-                add_bias_take_max(s)
+                add_bias(s)
             if tile_exists(s - 1):
                 exponentiate(s - 1)
             if tile_exists(s - 2):
@@ -383,11 +385,13 @@ def tile_swintransformer_pa_kernel(tc, x, q, k, wv, bv, pos_bias, out):
                 quantise_e(s - 4)
             if tile_exists(s - 1) and (s - 1) % QUAD == QUAD - 1:
                 invert_sums((s - 1) // QUAD)
-            if tile_exists(s - 5):
-                multiply_v(s - 5)
+            if tile_exists(s):
+                take_max(s)
             if tile_exists(s - 6):
                 scale_rows(s - 6)
             if tile_exists(s):
                 side_work(s)
             if tile_exists(s - 1):
                 turn_e(s - 1)
+            if tile_exists(s - 5):
+                multiply_v(s - 5)

@@ -28,6 +28,7 @@ HALVES = TOK // BANK
 QUAD = BANK // HD
 PAIRS = NW * HEADS
 N_TILES = PAIRS * TILES
+PIECE = HD // 2
 SCALE = 1.0 / math.sqrt(D)
 MASKED = -1.0e30
 
@@ -43,6 +44,7 @@ def tile_swintransformer_pa_kernel(tc, x, q, k, wv, bv, pos_bias, out):
         vkeep = ctx.enter_context(tc.tile_pool(name="vkeep", bufs=2))
         qk = ctx.enter_context(tc.tile_pool(name="qk", bufs=2))
         work = ctx.enter_context(tc.tile_pool(name="work", bufs=4))
+        handover = ctx.enter_context(tc.tile_pool(name="handover", bufs=1))
         stat = ctx.enter_context(tc.tile_pool(name="stat", bufs=6))
         ps_lg = ctx.enter_context(tc.psum_pool(name="ps_lg", bufs=4))
         ps_tr = ctx.enter_context(tc.psum_pool(name="ps_tr", bufs=2))
@@ -175,12 +177,12 @@ def tile_swintransformer_pa_kernel(tc, x, q, k, wv, bv, pos_bias, out):
         def add_bv(w, piece):
             if piece == 0:
                 px["v_grouped"] = proj.tile([P, PASSES, D, PACK], BF16, name="v_grouped", align_bytes=64)
-            g, h = divmod(piece, HEADS)
-            cols = slice(h * HD, (h + 1) * HD)
+            g, block = divmod(piece, D // PIECE)
+            cols = slice(block * PIECE, (block + 1) * PIECE)
             nc.gpsimd.tensor_tensor(
                 out=px["v_grouped"][:, g, cols, :],
                 in0=px["v_f32"][:, g * PACK : (g + 1) * PACK, cols].rearrange("p t c -> p c t"),
-                in1=bv_sb[:, cols].unsqueeze(2).to_broadcast([P, HD, PACK]),
+                in1=bv_sb[:, cols].unsqueeze(2).to_broadcast([P, PIECE, PACK]),
                 op=ALU.add,
             )
 
@@ -272,7 +274,7 @@ def tile_swintransformer_pa_kernel(tc, x, q, k, wv, bv, pos_bias, out):
             nc.scalar.copy(out=eT_planes[n][:], in_=eT_banks.pop(n)[:])
 
         def regroup_e(n):
-            e_groups[n] = work.tile([P, PASSES, P, PACK], BF16, name="e_grouped", align_bytes=64)
+            e_groups[n] = handover.tile([P, PASSES, P, PACK], BF16, name="e_grouped", align_bytes=64)
             nc.gpsimd.tensor_scalar(
                 out=e_groups[n][:],
                 in0=eT_planes.pop(n)[:].rearrange("p (g t) n -> p g n t", t=PACK),
@@ -348,8 +350,8 @@ def tile_swintransformer_pa_kernel(tc, x, q, k, wv, bv, pos_bias, out):
                     quantise_x(w + 1)
                 if h == 1:
                     project(w + 1, i)
-                if h == 2:
-                    add_bv(w + 1, i)
+                if h >= 2:
+                    add_bv(w + 1, (h - 2) * TILES + i)
             if h == 3 and i == 0 and w + 2 < NW:
                 load_x(w + 2)
 
@@ -363,7 +365,7 @@ def tile_swintransformer_pa_kernel(tc, x, q, k, wv, bv, pos_bias, out):
             mask_bias(0, i)
         for j in range(TILES):
             project(0, j)
-        for piece in range(TILES):
+        for piece in range(PASSES * D // PIECE):
             add_bv(0, piece)
 
         def tile_exists(n):
@@ -374,24 +376,25 @@ def tile_swintransformer_pa_kernel(tc, x, q, k, wv, bv, pos_bias, out):
                 multiply_qk(s + 1)
             if tile_exists(s):
                 add_bias(s)
+            if tile_exists(s - 3):
+                copy_eT(s - 3)
             if tile_exists(s - 1):
                 exponentiate(s - 1)
-            if tile_exists(s - 2):
-                copy_eT(s - 2)
-                regroup_e(s - 2)
             if tile_exists(s - 4):
                 if (s - 4) % (HEADS * TILES) == 0:
                     quantise_v((s - 4) // (HEADS * TILES))
                 quantise_e(s - 4)
-            if tile_exists(s - 1) and (s - 1) % QUAD == QUAD - 1:
-                invert_sums((s - 1) // QUAD)
+            if tile_exists(s - 2) and (s - 2) % QUAD == QUAD - 1:
+                invert_sums((s - 2) // QUAD)
             if tile_exists(s):
                 take_max(s)
+            if tile_exists(s - 3):
+                regroup_e(s - 3)
+            if tile_exists(s - 2):
+                turn_e(s - 2)
+            if tile_exists(s - 5):
+                multiply_v(s - 5)
             if tile_exists(s - 6):
                 scale_rows(s - 6)
             if tile_exists(s):
                 side_work(s)
-            if tile_exists(s - 1):
-                turn_e(s - 1)
-            if tile_exists(s - 5):
-                multiply_v(s - 5)

@@ -28,6 +28,7 @@ HALVES = TOK // BANK
 QUAD = BANK // HD
 PAIRS = NW * HEADS
 N_TILES = PAIRS * TILES
+ROWS = 2 * P // WIN
 PIECE = HD // 2
 SCALE = 1.0 / math.sqrt(D)
 MASKED = -1.0e30
@@ -44,7 +45,6 @@ def tile_swintransformer_pa_kernel(tc, x, q, k, wv, bv, pos_bias, out):
         vkeep = ctx.enter_context(tc.tile_pool(name="vkeep", bufs=2))
         qk = ctx.enter_context(tc.tile_pool(name="qk", bufs=2))
         work = ctx.enter_context(tc.tile_pool(name="work", bufs=4))
-        handover = ctx.enter_context(tc.tile_pool(name="handover", bufs=1))
         stat = ctx.enter_context(tc.tile_pool(name="stat", bufs=6))
         ps_lg = ctx.enter_context(tc.psum_pool(name="ps_lg", bufs=4))
         ps_tr = ctx.enter_context(tc.psum_pool(name="ps_tr", bufs=2))
@@ -88,12 +88,12 @@ def tile_swintransformer_pa_kernel(tc, x, q, k, wv, bv, pos_bias, out):
 
         def load_x(w):
             wi, wj = divmod(w, GRID)
-            rows_per_tile = P // WIN
             pixels = x[0, wi * WIN : (wi + 1) * WIN, wj * WIN : (wj + 1) * WIN, :]
-            by_row = pixels.rearrange("(j r) c d -> r c j d", r=rows_per_tile)
+            by_row = pixels.rearrange("(a r) (c e) d -> r c a (e d)", r=ROWS, e=2)
             tile_x = xin.tile([P, TILES, D], BF16, name="x_raw")
-            for r in range(rows_per_tile):
-                nc.sync.dma_start(out=tile_x[r * WIN : (r + 1) * WIN, :, :], in_=by_row[r])
+            slots = tile_x[:].rearrange("p (a e) d -> p a (e d)", e=2)
+            for r in range(ROWS):
+                nc.sync.dma_start(out=slots[r * (WIN // 2) : (r + 1) * (WIN // 2), :, :], in_=by_row[r])
             x_raw[w] = tile_x
 
         load_x(0)
@@ -202,7 +202,6 @@ def tile_swintransformer_pa_kernel(tc, x, q, k, wv, bv, pos_bias, out):
         sums = {}
         e_rows = {}
         eT_banks = {}
-        eT_planes = {}
         e_groups = {}
         weights = {}
         o_banks = {}
@@ -264,24 +263,16 @@ def tile_swintransformer_pa_kernel(tc, x, q, k, wv, bv, pos_bias, out):
             sums[group] = recip
 
         def turn_e(n):
-            e = e_rows.pop(n)
-            eT_banks[n] = ps_tr.tile([P, TILES, P], BF16, name="eT_ps", tag="tr")
-            for j in range(TILES):
-                nc.tensor.transpose(out=eT_banks[n][:, j, :], in_=e[:, j * P : (j + 1) * P], identity=ident_bf[:])
+            words = e_rows.pop(n)[:].bitcast(F32)
+            eT_banks[n] = ps_tr.tile([P, TILES // 2, P], F32, name="eT_ps", tag="tr")
+            for a in range(TILES // 2):
+                nc.tensor.transpose(out=eT_banks[n][:, a, :], in_=words[:, a * P : (a + 1) * P], identity=ident_f32[:])
 
         def copy_eT(n):
-            eT_planes[n] = work.tile([P, TILES, P], BF16, name="eT")
-            nc.scalar.copy(out=eT_planes[n][:], in_=eT_banks.pop(n)[:])
-
-        def regroup_e(n):
-            e_groups[n] = handover.tile([P, PASSES, P, PACK], BF16, name="e_grouped", align_bytes=64)
-            nc.gpsimd.tensor_scalar(
-                out=e_groups[n][:],
-                in0=eT_planes.pop(n)[:].rearrange("p (g t) n -> p g n t", t=PACK),
-                scalar1=1.0,
-                scalar2=0.0,
-                op0=ALU.mult,
-                op1=ALU.add,
+            e_groups[n] = work.tile([P, PASSES, P, PACK], BF16, name="e_grouped", align_bytes=64)
+            nc.scalar.copy(
+                out=e_groups[n][:].bitcast(F32),
+                in_=eT_banks.pop(n)[:].rearrange("p (g u) n -> p g n u", u=2),
             )
 
         def quantise_e(n):
@@ -388,8 +379,6 @@ def tile_swintransformer_pa_kernel(tc, x, q, k, wv, bv, pos_bias, out):
                 invert_sums((s - 2) // QUAD)
             if tile_exists(s):
                 take_max(s)
-            if tile_exists(s - 3):
-                regroup_e(s - 3)
             if tile_exists(s - 2):
                 turn_e(s - 2)
             if tile_exists(s - 5):

@@ -11,6 +11,7 @@ U8 = mybir.dt.uint8
 FP8X4 = mybir.dt.float8_e4m3fn_x4
 ALU = mybir.AluOpType
 ACT = mybir.ActivationFunctionType
+AXIS = mybir.AxisListType
 
 P = 128
 PACK = 4
@@ -29,9 +30,12 @@ QUAD = BANK // HD
 PAIRS = NW * HEADS
 N_TILES = PAIRS * TILES
 ROWS = 2 * P // WIN
-PIECE = HD // 2
 SCALE = 1.0 / math.sqrt(D)
+UNSCALE = math.sqrt(D)
 MASKED = -1.0e30
+LAG = 6
+HEAD_STEPS = 5
+V_SLOTS = 10
 
 FLOPS = 2 * NW * TOK * D * D + 2 * (2 * PAIRS * TOK * TOK * HD)
 
@@ -40,15 +44,18 @@ def tile_swintransformer_pa_kernel(tc, x, q, k, wv, bv, pos_bias, out):
     nc = tc.nc
     with ExitStack() as ctx:
         const = ctx.enter_context(tc.tile_pool(name="const", bufs=1))
+        bias_in = ctx.enter_context(tc.tile_pool(name="bias_in", bufs=3))
+        bias_keep = ctx.enter_context(tc.tile_pool(name="bias_keep", bufs=2))
         xin = ctx.enter_context(tc.tile_pool(name="xin", bufs=2))
         proj = ctx.enter_context(tc.tile_pool(name="proj", bufs=1))
-        vkeep = ctx.enter_context(tc.tile_pool(name="vkeep", bufs=2))
+        vkeep = ctx.enter_context(tc.tile_pool(name="vkeep", bufs=NW))
         qk = ctx.enter_context(tc.tile_pool(name="qk", bufs=2))
-        work = ctx.enter_context(tc.tile_pool(name="work", bufs=4))
+        work = ctx.enter_context(tc.tile_pool(name="work", bufs=3))
+        coded = ctx.enter_context(tc.tile_pool(name="coded", bufs=LAG))
         stat = ctx.enter_context(tc.tile_pool(name="stat", bufs=6))
         ps_lg = ctx.enter_context(tc.psum_pool(name="ps_lg", bufs=4))
-        ps_tr = ctx.enter_context(tc.psum_pool(name="ps_tr", bufs=2))
-        ps_o = ctx.enter_context(tc.psum_pool(name="ps_o", bufs=2))
+        ps_tr = ctx.enter_context(tc.psum_pool(name="ps_tr", bufs=3))
+        ps_o = ctx.enter_context(tc.psum_pool(name="ps_o", bufs=1))
         ctx.enter_context(tc.manual_schedule())
 
         ident_bf = const.tile([P, P], BF16, name="ident_bf")
@@ -56,24 +63,50 @@ def tile_swintransformer_pa_kernel(tc, x, q, k, wv, bv, pos_bias, out):
         ident_f32 = const.tile([P, P], F32, name="ident_f32")
         make_identity(nc, ident_f32[:])
 
+        later_scalar = []
+        later_vector = []
+
+        def run_all(calls):
+            for call in list(calls):
+                call()
+            calls.clear()
+
         raw = {}
+        turned = {}
 
         def load_qk(m):
-            w, h = divmod(m, HEADS)
+            h, w = divmod(m, NW)
             q_raw = qk.tile([P, TILES, HD], BF16, name="q_raw")
             nc.sync.dma_start(out=q_raw[:], in_=q[0, w, h].rearrange("(i p) d -> p i d", p=P))
             k_raw = qk.tile([P, TILES, HD], BF16, name="k_raw")
             nc.sync.dma_start(out=k_raw[:], in_=k[0, w, h].rearrange("(i p) d -> p i d", p=P))
             raw[m] = {"q": q_raw, "k": k_raw}
 
-        bias = [const.tile([P, TILES, TOK], BF16, name="bias%d" % h) for h in range(HEADS)]
-
-        def load_bias(h):
+        def transpose_qk(m, which):
+            source = raw[m].pop(which)
+            turned_ps = ps_tr.tile([P, TILES, P], BF16, name="turned_ps", tag="tr")
             for i in range(TILES):
-                nc.sync.dma_start(out=bias[h][:, i, :], in_=pos_bias[h, i * P : (i + 1) * P, :])
+                nc.tensor.transpose(out=turned_ps[:, i, :], in_=source[:, i, :], identity=ident_bf[:])
 
-        def mask_bias(h, i):
-            block = bias[h][:, i, i * P : (i + 1) * P]
+            def copy_out():
+                turned_sb = qk.tile([P, TILES, P], BF16, name=which + "T")
+                nc.scalar.copy(out=turned_sb[:], in_=turned_ps[:])
+                turned[(m, which)] = turned_sb
+
+            later_scalar.append(copy_out)
+
+        units = [(h, i) for h in range(HEADS) for i in range(TILES)]
+        bias_raw = {}
+        biasT = {}
+
+        def load_bias(u):
+            h, i = units[u]
+            bias_raw[u] = bias_in.tile([P, TOK], BF16, name="bias_raw")
+            nc.sync.dma_start(out=bias_raw[u][:], in_=pos_bias[h, i * P : (i + 1) * P, :])
+
+        def mask_bias(u):
+            h, i = units[u]
+            block = bias_raw[u][:, i * P : (i + 1) * P]
             nc.gpsimd.affine_select(
                 out=block,
                 in_=block,
@@ -84,7 +117,25 @@ def tile_swintransformer_pa_kernel(tc, x, q, k, wv, bv, pos_bias, out):
                 channel_multiplier=1,
             )
 
+        def turn_bias(u):
+            h, i = units[u]
+            source = bias_raw.pop(u)
+            bT_ps = ps_tr.tile([P, TILES, P], BF16, name="bT_ps", tag="tr")
+            for j in range(TILES):
+                nc.tensor.transpose(out=bT_ps[:, j, :], in_=source[:, j * P : (j + 1) * P], identity=ident_bf[:])
+
+            def copy_out():
+                if i == 0:
+                    biasT[h] = bias_keep.tile([P, TILES, TOK], F32, name="biasT")
+                nc.scalar.activation(
+                    out=biasT[h][:, :, i * P : (i + 1) * P], in_=bT_ps[:], func=ACT.Copy, scale=UNSCALE
+                )
+
+            later_scalar.append(copy_out)
+
         x_raw = {}
+        px = {}
+        values = {}
 
         def load_x(w):
             wi, wj = divmod(w, GRID)
@@ -96,72 +147,42 @@ def tile_swintransformer_pa_kernel(tc, x, q, k, wv, bv, pos_bias, out):
                 nc.sync.dma_start(out=slots[r * (WIN // 2) : (r + 1) * (WIN // 2), :, :], in_=by_row[r])
             x_raw[w] = tile_x
 
-        load_x(0)
-        w_raw = const.tile([P, PACK, D], BF16, name="w_raw")
-        nc.sync.dma_start(
-            out=w_raw[:].rearrange("p (u e) n -> p u (e n)", e=2),
-            in_=wv.rearrange("(u p e) n -> p u (e n)", u=2, e=2),
-        )
-        load_qk(0)
-        load_bias(0)
-        bv_sb = const.tile([P, D], BF16, name="bv_sb")
-        nc.sync.dma_start(out=bv_sb[:], in_=bv.partition_broadcast(P))
-        load_qk(1)
-        load_bias(1)
-        load_x(1)
-
-        w_grouped = const.tile([P, D, PACK], BF16, name="w_grouped", align_bytes=64)
-        nc.vector.tensor_copy(out=w_grouped[:], in_=w_raw[:].rearrange("p t n -> p n t"))
-        w_codes = const.tile([P, D], U32, name="w_codes", align_bytes=64)
-        w_scales = const.tile([P, D], U8, name="w_scales", align_bytes=64)
-        nc.vector.quantize_mx(
-            out=w_codes[:].bitcast(FP8X4),
-            scales=w_scales[:],
-            in_=w_grouped[:].rearrange("p n t -> p (n t)"),
-        )
-
-        turned = {}
-
-        def transpose_qk(m, which):
-            source = raw[m].pop(which)
-            turned_ps = ps_tr.tile([P, TILES, P], BF16, name="turned_ps", tag="tr")
-            for i in range(TILES):
-                nc.tensor.transpose(out=turned_ps[:, i, :], in_=source[:, i, :], identity=ident_bf[:])
-            turned_sb = qk.tile([P, TILES, P], BF16, name=which + "T")
-            nc.scalar.copy(out=turned_sb[:], in_=turned_ps[:])
-            turned[(m, which)] = turned_sb
-
-        px = {}
-        values = {}
-
         def turn_x(w, j):
             if j == 0:
                 px["grouped"] = proj.tile([P, TILES, P, PACK], BF16, name="x_grouped", align_bytes=64)
-            xT_ps = ps_lg.tile([P, 2, 2, P], F32, name="xT_ps", tag="lg")
+            grouped = px["grouped"]
+            xT_ps = ps_tr.tile([P, 2, 2, P], F32, name="xT_ps", tag="tr")
             for jj in range(2):
                 words = x_raw[w][:, j + jj, :].bitcast(F32)
                 for u in range(2):
                     nc.tensor.transpose(
                         out=xT_ps[:, jj, u, :], in_=words[:, u * P : (u + 1) * P], identity=ident_f32[:]
                     )
-            nc.scalar.copy(
-                out=px["grouped"][:].bitcast(F32)[:, j : j + 2, :, :],
-                in_=xT_ps[:].rearrange("p j u k -> p j k u"),
-            )
 
-        def quantise_x(w):
-            x_raw.pop(w)
-            px["codes"] = proj.tile([P, TOK], U32, name="x_codes", align_bytes=64)
-            px["scales"] = proj.tile([P, TOK], U8, name="x_scales", align_bytes=64)
+            def copy_out():
+                nc.scalar.copy(
+                    out=grouped[:].bitcast(F32)[:, j : j + 2, :, :],
+                    in_=xT_ps[:].rearrange("p j u k -> p j k u"),
+                )
+
+            later_scalar.append(copy_out)
+
+        def quantise_x(w, g):
+            if g == 0:
+                px["codes"] = proj.tile([P, TOK], U32, name="x_codes", align_bytes=64)
+                px["scales"] = proj.tile([P, TOK], U8, name="x_scales", align_bytes=64)
+            tokens = slice(g * BANK, (g + 1) * BANK)
             nc.vector.quantize_mx(
-                out=px["codes"][:].bitcast(FP8X4),
-                scales=px["scales"][:],
-                in_=px["grouped"][:].rearrange("p j k t -> p (j k t)"),
+                out=px["codes"][:, tokens].bitcast(FP8X4),
+                scales=px["scales"][:, tokens],
+                in_=px["grouped"][:, g * PACK : (g + 1) * PACK, :, :].rearrange("p j k t -> p (j k t)"),
             )
-            px["v_f32"] = proj.tile([P, TILES, D], F32, name="v_f32")
 
         def project(w, j):
-            v_ps = ps_lg.tile([P, D], F32, name="v_ps", tag="lg")
+            if j == 0:
+                px["v_bf"] = proj.tile([P, TILES, D], BF16, name="v_bf")
+            v_bf = px["v_bf"]
+            v_ps = ps_tr.tile([P, D], F32, name="v_ps", tag="tr")
             tokens = slice(j * P, (j + 1) * P)
             nc.tensor.matmul_mx(
                 out=v_ps[:],
@@ -172,95 +193,120 @@ def tile_swintransformer_pa_kernel(tc, x, q, k, wv, bv, pos_bias, out):
                 start=True,
                 stop=True,
             )
-            nc.scalar.copy(out=px["v_f32"][:, j, :], in_=v_ps[:])
 
-        def add_bv(w, piece):
-            if piece == 0:
+            def add_bv():
+                nc.vector.tensor_tensor(out=v_bf[:, j, :], in0=v_ps[:], in1=bv_sb[:], op=ALU.add)
+
+            later_vector.append(add_bv)
+
+        def group_v(w, g):
+            if g == 0:
                 px["v_grouped"] = proj.tile([P, PASSES, D, PACK], BF16, name="v_grouped", align_bytes=64)
-            g, block = divmod(piece, D // PIECE)
-            cols = slice(block * PIECE, (block + 1) * PIECE)
-            nc.gpsimd.tensor_tensor(
-                out=px["v_grouped"][:, g, cols, :],
-                in0=px["v_f32"][:, g * PACK : (g + 1) * PACK, cols].rearrange("p t c -> p c t"),
-                in1=bv_sb[:, cols].unsqueeze(2).to_broadcast([P, PIECE, PACK]),
-                op=ALU.add,
-            )
+            for half in range(2):
+                cols = slice(half * D // 2, (half + 1) * D // 2)
+                nc.gpsimd.tensor_scalar(
+                    out=px["v_grouped"][:, g, cols, :],
+                    in0=px["v_bf"][:, g * PACK : (g + 1) * PACK, cols].rearrange("p t c -> p c t"),
+                    scalar1=1.0,
+                    scalar2=0.0,
+                    op0=ALU.mult,
+                    op1=ALU.add,
+                )
 
-        def quantise_v(w):
-            v_codes = vkeep.tile([P, PASSES, D], U32, name="v_codes", align_bytes=64)
-            v_scales = vkeep.tile([P, PASSES, D], U8, name="v_scales", align_bytes=64)
+        def quantise_v(w, g):
+            if g == 0:
+                v_codes = vkeep.tile([P, PASSES, D], U32, name="v_codes", align_bytes=64)
+                v_scales = vkeep.tile([P, PASSES, D], U8, name="v_scales", align_bytes=64)
+                values[w] = (v_codes, v_scales)
+            v_codes, v_scales = values[w]
             nc.vector.quantize_mx(
-                out=v_codes[:].rearrange("p g c -> p (g c)").bitcast(FP8X4),
-                scales=v_scales[:].rearrange("p g c -> p (g c)"),
-                in_=px["v_grouped"][:].rearrange("p g c t -> p (g c t)"),
+                out=v_codes[:, g, :].bitcast(FP8X4),
+                scales=v_scales[:, g, :],
+                in_=px["v_grouped"][:, g, :, :].rearrange("p c t -> p (c t)"),
             )
-            values[w] = (v_codes, v_scales)
 
-        qk_banks = {}
-        logits = {}
+        lg_banks = {}
+        maxima = {}
         neg_max = {}
         sums = {}
+        recips = {}
         e_rows = {}
         eT_banks = {}
         e_groups = {}
         weights = {}
         o_banks = {}
-        o_rows = {}
 
-        def multiply_qk(n):
+        def place(n):
             m, i = divmod(n, TILES)
+            h, w = divmod(m, NW)
+            return m, h, w, i
+
+        def fill_logits(n):
+            m, h, w, i = place(n)
             qT, kT = turned[(m, "q")], turned[(m, "k")]
-            qk_banks[n] = []
+            lg_banks[n] = []
             for c in range(HALVES):
-                qk_ps = ps_lg.tile([P, BANK], F32, name="qk_ps", tag="lg")
+                lg_ps = ps_lg.tile([P, BANK], F32, name="lg_ps", tag="lg")
                 nc.tensor.matmul(
-                    out=qk_ps[:],
+                    out=lg_ps[:],
                     lhsT=qT[:, i, :],
                     rhs=kT[:].rearrange("d j p -> d (j p)")[:, c * BANK : (c + 1) * BANK],
                     start=True,
-                    stop=True,
+                    stop=False,
                 )
-                qk_banks[n].append(qk_ps)
-
-        def add_bias(n):
-            m, i = divmod(n, TILES)
-            h = m % HEADS
-            logits[n] = work.tile([P, TOK], F32, name="logits")
-            for c, qk_ps in enumerate(qk_banks.pop(n)):
-                keys = slice(c * BANK, (c + 1) * BANK)
-                nc.vector.scalar_tensor_tensor(
-                    out=logits[n][:, keys],
-                    in0=qk_ps[:],
-                    scalar=SCALE,
-                    in1=bias[h][:, i, keys],
-                    op0=ALU.mult,
-                    op1=ALU.add,
-                )
+                lg_banks[n].append(lg_ps)
+            for c in range(HALVES):
+                for jj in range(QUAD):
+                    nc.tensor.matmul(
+                        out=lg_banks[n][c][:, jj * P : (jj + 1) * P],
+                        lhsT=biasT[h][:, c * QUAD + jj, i * P : (i + 1) * P],
+                        rhs=ident_f32[:],
+                        is_transpose=True,
+                        start=False,
+                        stop=(jj == QUAD - 1),
+                    )
 
         def take_max(n):
+            maxima[n] = stat.tile([P, HALVES], F32, name="maxima")
+            for c in range(HALVES):
+                nc.vector.tensor_reduce(out=maxima[n][:, c : c + 1], in_=lg_banks[n][c][:], axis=AXIS.X, op=ALU.max)
+
+        def finish_max(n):
+            both = maxima.pop(n)
             neg_max[n] = stat.tile([P, 1], F32, name="neg_max")
-            nc.vector.tensor_reduce(
-                out=neg_max[n][:], in_=logits[n][:], axis=mybir.AxisListType.X, op=ALU.max, negate=True
+            nc.vector.tensor_scalar(
+                out=neg_max[n][:],
+                in0=both[:, 0:1],
+                scalar1=both[:, 1:2],
+                scalar2=-SCALE,
+                op0=ALU.max,
+                op1=ALU.mult,
             )
 
         def exponentiate(n):
             group, r = divmod(n, QUAD)
             if r == 0:
-                sums[group] = stat.tile([P, QUAD], F32, name="rowsum")
+                sums[group] = stat.tile([P, QUAD, HALVES], F32, name="rowsum")
             e_rows[n] = work.tile([P, TOK], BF16, name="e")
-            nc.scalar.activation(
-                out=e_rows[n][:],
-                in_=logits.pop(n)[:],
-                func=ACT.Exp,
-                bias=neg_max.pop(n)[:],
-                scale=1.0,
-                accum_out=sums[group][:, r : r + 1],
-            )
+            shift = neg_max.pop(n)
+            for c, lg_ps in enumerate(lg_banks.pop(n)):
+                nc.scalar.activation(
+                    out=e_rows[n][:, c * BANK : (c + 1) * BANK],
+                    in_=lg_ps[:],
+                    func=ACT.Exp,
+                    bias=shift[:],
+                    scale=SCALE,
+                    accum_out=sums[group][:, r, c : c + 1],
+                )
+
+        def add_sums(group):
+            total = stat.tile([P, QUAD], F32, name="total")
+            nc.vector.tensor_reduce(out=total[:], in_=sums.pop(group)[:], axis=AXIS.X, op=ALU.add)
+            sums[group] = total
 
         def invert_sums(group):
-            recip = stat.tile([P, QUAD], F32, name="recip")
-            nc.vector.reciprocal(out=recip[:], in_=sums[group][:])
-            sums[group] = recip
+            recips[group] = stat.tile([P, QUAD], F32, name="recip")
+            nc.vector.reciprocal(out=recips[group][:], in_=sums.pop(group)[:])
 
         def turn_e(n):
             words = e_rows.pop(n)[:].bitcast(F32)
@@ -276,8 +322,8 @@ def tile_swintransformer_pa_kernel(tc, x, q, k, wv, bv, pos_bias, out):
             )
 
         def quantise_e(n):
-            e_codes = work.tile([P, PASSES * P], U32, name="e_codes", align_bytes=64)
-            e_scales = work.tile([P, PASSES * P], U8, name="e_scales", align_bytes=64)
+            e_codes = coded.tile([P, PASSES * P], U32, name="e_codes", align_bytes=64)
+            e_scales = coded.tile([P, PASSES * P], U8, name="e_scales", align_bytes=64)
             nc.vector.quantize_mx(
                 out=e_codes[:].bitcast(FP8X4),
                 scales=e_scales[:],
@@ -286,104 +332,144 @@ def tile_swintransformer_pa_kernel(tc, x, q, k, wv, bv, pos_bias, out):
             weights[n] = (e_codes, e_scales)
 
         def multiply_v(n):
-            v_codes, v_scales = values[n // (HEADS * TILES)]
+            m, h, w, i = place(n)
+            group, r = divmod(n, QUAD)
+            v_codes, v_scales = values[w]
             e_codes, e_scales = weights.pop(n)
-            o_banks[n] = ps_o.tile([P, D], F32, name="o_ps")
+            if r == 0:
+                o_banks[group] = ps_o.tile([P, QUAD, HD], F32, name="o_ps")
+            cols = slice(h * HD, (h + 1) * HD)
             for g in range(PASSES):
                 queries = slice(g * P, (g + 1) * P)
                 nc.tensor.matmul_mx(
-                    out=o_banks[n][:],
+                    out=o_banks[group][:, r, :],
                     lhsT=e_codes[:, queries].bitcast(FP8X4),
                     lhsT_scale=e_scales[:, queries],
-                    rhs=v_codes[:, g, :].bitcast(FP8X4),
-                    rhs_scale=v_scales[:, g, :],
+                    rhs=v_codes[:, g, cols].bitcast(FP8X4),
+                    rhs_scale=v_scales[:, g, cols],
                     start=(g == 0),
                     stop=(g == PASSES - 1),
                 )
 
-        def scale_rows(n):
-            m, i = divmod(n, TILES)
-            w, h = divmod(m, HEADS)
-            group, r = divmod(n, QUAD)
-            if r == 0:
-                o_rows[group] = work.tile([P, QUAD, HD], F32, name="o_sb")
-            cols = slice(h * HD, (h + 1) * HD)
-            nc.scalar.activation(
-                out=o_rows[group][:, r, :],
-                in_=o_banks.pop(n)[:, cols],
-                func=ACT.Copy,
-                scale=sums[group][:, r : r + 1],
+        def normalise(group):
+            m, h, w, i = place(group * QUAD)
+            o_sb = work.tile([P, QUAD, HD], F32, name="o_sb")
+            nc.vector.tensor_tensor(
+                out=o_sb[:],
+                in0=o_banks.pop(group)[:],
+                in1=recips.pop(group)[:].unsqueeze(2).to_broadcast([P, QUAD, HD]),
+                op=ALU.mult,
             )
-            if r == QUAD - 1:
-                nc.sync.dma_start(
-                    out=out[0, w].rearrange("(i p) c -> p i c", p=P)[:, i - r : i + 1, cols],
-                    in_=o_rows.pop(group)[:],
-                )
-                sums.pop(group)
+            nc.sync.dma_start(
+                out=out[0, w].rearrange("(i p) c -> p i c", p=P)[:, i : i + QUAD, h * HD : (h + 1) * HD],
+                in_=o_sb[:],
+            )
 
-        def side_work(n):
-            m, i = divmod(n, TILES)
-            w, h = divmod(m, HEADS)
-            if i == 0 and m + 2 < PAIRS:
-                load_qk(m + 2)
-            if i == 2 and m + 1 < PAIRS:
-                transpose_qk(m + 1, "q")
-            if i == 4 and m + 1 < PAIRS:
-                transpose_qk(m + 1, "k")
-            if w == 0 and i == 0 and h + 2 < HEADS:
-                load_bias(h + 2)
-            if w == 0 and h + 1 < HEADS:
-                mask_bias(h + 1, i)
-            if w + 1 < NW:
-                if h == 0 and i >= TILES // 2:
-                    turn_x(w + 1, 2 * (i - TILES // 2))
-                if h == 1 and i == 0:
-                    quantise_x(w + 1)
-                if h == 1:
-                    project(w + 1, i)
-                if h >= 2:
-                    add_bv(w + 1, (h - 2) * TILES + i)
-            if h == 3 and i == 0 and w + 2 < NW:
-                load_x(w + 2)
+        unit_at = {}
+        for u, (h, i) in enumerate(units):
+            unit_at[i - 3 if h == 0 else (h - 1) * NW * TILES + 7 + 3 * i] = u
 
-        for j in range(0, TILES, 2):
-            turn_x(0, j)
-        quantise_x(0)
-        transpose_qk(0, "q")
-        transpose_qk(0, "k")
-        multiply_qk(0)
-        for i in range(TILES):
-            mask_bias(0, i)
-        for j in range(TILES):
-            project(0, j)
-        for piece in range(PASSES * D // PIECE):
-            add_bv(0, piece)
+        def v_slot(w, s):
+            return s - (w * TILES + LAG - (V_SLOTS - 1))
+
+        def vector_side(s):
+            for w in range(NW):
+                slot = v_slot(w, s)
+                if slot in (2, 3):
+                    quantise_x(w, slot - 2)
+                if slot in (7, 9):
+                    quantise_v(w, (slot - 7) // 2)
+
+        def transposes_side(s):
+            m, i = divmod(s + HEAD_STEPS, TILES)
+            if m < PAIRS and i == 0:
+                transpose_qk(m, "q")
+            if m < PAIRS and i == 1:
+                transpose_qk(m, "k")
+                if m + 2 < PAIRS:
+                    load_qk(m + 2)
+            if s in unit_at:
+                u = unit_at[s]
+                turn_bias(u)
+                if u + 1 < len(units):
+                    mask_bias(u + 1)
+                if u + 3 < len(units):
+                    load_bias(u + 3)
+            for w in range(NW):
+                slot = v_slot(w, s)
+                if slot in (0, 1):
+                    turn_x(w, 4 * slot)
+                    turn_x(w, 4 * slot + 2)
+                if slot == 2:
+                    x_raw.pop(w)
+                    if w + 2 < NW:
+                        load_x(w + 2)
+
+        def mx_side(s):
+            for w in range(NW):
+                slot = v_slot(w, s)
+                if 2 <= slot <= 5:
+                    project(w, 2 * (slot - 2))
+                    project(w, 2 * (slot - 2) + 1)
+                if slot in (5, 7):
+                    group_v(w, (slot - 5) // 2)
+
+        load_qk(0)
+        load_bias(0)
+        load_x(0)
+        w_raw = const.tile([P, PACK, D], BF16, name="w_raw")
+        nc.sync.dma_start(
+            out=w_raw[:].rearrange("p (u e) n -> p u (e n)", e=2),
+            in_=wv.rearrange("(u p e) n -> p u (e n)", u=2, e=2),
+        )
+        bv_sb = const.tile([P, D], BF16, name="bv_sb")
+        nc.sync.dma_start(out=bv_sb[:], in_=bv.partition_broadcast(P))
+        load_bias(1)
+        load_bias(2)
+        load_qk(1)
+        load_x(1)
+        mask_bias(0)
+
+        w_grouped = const.tile([P, D, PACK], BF16, name="w_grouped", align_bytes=64)
+        nc.vector.tensor_copy(out=w_grouped[:], in_=w_raw[:].rearrange("p t n -> p n t"))
+        w_codes = const.tile([P, D], U32, name="w_codes", align_bytes=64)
+        w_scales = const.tile([P, D], U8, name="w_scales", align_bytes=64)
+        nc.vector.quantize_mx(
+            out=w_codes[:].bitcast(FP8X4),
+            scales=w_scales[:],
+            in_=w_grouped[:].rearrange("p n t -> p (n t)"),
+        )
 
         def tile_exists(n):
             return 0 <= n < N_TILES
 
-        for s in range(N_TILES + 7):
+        def group_due(n):
+            return tile_exists(n) and n % QUAD == QUAD - 1
+
+        for s in range(-HEAD_STEPS, N_TILES + LAG + 1):
             if tile_exists(s + 1):
-                multiply_qk(s + 1)
+                fill_logits(s + 1)
             if tile_exists(s):
-                add_bias(s)
-            if tile_exists(s - 3):
-                copy_eT(s - 3)
-            if tile_exists(s - 1):
-                exponentiate(s - 1)
-            if tile_exists(s - 4):
-                if (s - 4) % (HEADS * TILES) == 0:
-                    quantise_v((s - 4) // (HEADS * TILES))
-                quantise_e(s - 4)
-            if tile_exists(s - 2) and (s - 2) % QUAD == QUAD - 1:
-                invert_sums((s - 2) // QUAD)
-            if tile_exists(s):
-                take_max(s)
+                exponentiate(s)
+            run_all(later_vector)
             if tile_exists(s - 2):
-                turn_e(s - 2)
-            if tile_exists(s - 5):
-                multiply_v(s - 5)
-            if tile_exists(s - 6):
-                scale_rows(s - 6)
-            if tile_exists(s):
-                side_work(s)
+                quantise_e(s - 2)
+            vector_side(s)
+            if group_due(s - 1):
+                add_sums((s - 1) // QUAD)
+            if group_due(s - LAG - 1):
+                normalise((s - LAG - 1) // QUAD)
+            if group_due(s - 2):
+                invert_sums((s - 2) // QUAD)
+            if tile_exists(s + 1):
+                take_max(s + 1)
+                finish_max(s + 1)
+            if tile_exists(s - 1):
+                turn_e(s - 1)
+            run_all(later_scalar)
+            if tile_exists(s - 1):
+                copy_eT(s - 1)
+            transposes_side(s)
+            if tile_exists(s - LAG):
+                multiply_v(s - LAG)
+            mx_side(s)

@@ -127,11 +127,11 @@ def tile_swintransformer_pa_kernel(tc, x, q, k, wv, bv, pos_bias, out):
             def copy_out():
                 if i == 0:
                     biasT[h] = bias_keep.tile([P, TILES, TOK], F32, name="biasT")
-                nc.scalar.activation(
-                    out=biasT[h][:, :, i * P : (i + 1) * P], in_=bT_ps[:], func=ACT.Copy, scale=UNSCALE
+                nc.vector.tensor_scalar(
+                    out=biasT[h][:, :, i * P : (i + 1) * P], in0=bT_ps[:], scalar1=UNSCALE, scalar2=None, op0=ALU.mult
                 )
 
-            later_scalar.append(copy_out)
+            later_vector.append(copy_out)
 
         x_raw = {}
         px = {}
@@ -226,7 +226,6 @@ def tile_swintransformer_pa_kernel(tc, x, q, k, wv, bv, pos_bias, out):
             )
 
         lg_banks = {}
-        maxima = {}
         neg_max = {}
         sums = {}
         recips = {}
@@ -266,22 +265,19 @@ def tile_swintransformer_pa_kernel(tc, x, q, k, wv, bv, pos_bias, out):
                         stop=(jj == QUAD - 1),
                     )
 
-        def take_max(n):
-            maxima[n] = stat.tile([P, HALVES], F32, name="maxima")
-            for c in range(HALVES):
-                nc.vector.tensor_reduce(out=maxima[n][:, c : c + 1], in_=lg_banks[n][c][:], axis=AXIS.X, op=ALU.max)
-
-        def finish_max(n):
-            both = maxima.pop(n)
-            neg_max[n] = stat.tile([P, 1], F32, name="neg_max")
+        def take_max(n, c):
+            unused = work.tile([P, BANK], BF16, name="unused")
+            lowest = stat.tile([P, 1], F32, name="lowest%d" % c)
             nc.vector.tensor_scalar(
-                out=neg_max[n][:],
-                in0=both[:, 0:1],
-                scalar1=both[:, 1:2],
-                scalar2=-SCALE,
-                op0=ALU.max,
-                op1=ALU.mult,
+                out=unused[:],
+                in0=lg_banks[n][c][:],
+                scalar1=-SCALE,
+                scalar2=(None if c == 0 else neg_max[n][:]),
+                op0=ALU.mult,
+                op1=ALU.min,
+                accum_out=lowest[:],
             )
+            neg_max[n] = lowest
 
         def exponentiate(n):
             group, r = divmod(n, QUAD)
@@ -452,8 +448,6 @@ def tile_swintransformer_pa_kernel(tc, x, q, k, wv, bv, pos_bias, out):
             if tile_exists(s):
                 exponentiate(s)
             run_all(later_vector)
-            if tile_exists(s - 2):
-                quantise_e(s - 2)
             vector_side(s)
             if group_due(s - 1):
                 add_sums((s - 1) // QUAD)
@@ -462,8 +456,11 @@ def tile_swintransformer_pa_kernel(tc, x, q, k, wv, bv, pos_bias, out):
             if group_due(s - 2):
                 invert_sums((s - 2) // QUAD)
             if tile_exists(s + 1):
-                take_max(s + 1)
-                finish_max(s + 1)
+                take_max(s + 1, 0)
+            if tile_exists(s - 2):
+                quantise_e(s - 2)
+            if tile_exists(s + 1):
+                take_max(s + 1, 1)
             if tile_exists(s - 1):
                 turn_e(s - 1)
             run_all(later_scalar)

@@ -45,6 +45,7 @@ def tile_swintransformer_pa_kernel(tc, x, q, k, wv, bv, pos_bias, out):
     with ExitStack() as ctx:
         const = ctx.enter_context(tc.tile_pool(name="const", bufs=1))
         bias_in = ctx.enter_context(tc.tile_pool(name="bias_in", bufs=3))
+        bias_mid = ctx.enter_context(tc.tile_pool(name="bias_mid", bufs=2))
         bias_keep = ctx.enter_context(tc.tile_pool(name="bias_keep", bufs=2))
         xin = ctx.enter_context(tc.tile_pool(name="xin", bufs=2))
         proj = ctx.enter_context(tc.tile_pool(name="proj", bufs=1))
@@ -79,7 +80,10 @@ def tile_swintransformer_pa_kernel(tc, x, q, k, wv, bv, pos_bias, out):
             q_raw = qk.tile([P, TILES, HD], BF16, name="q_raw")
             nc.sync.dma_start(out=q_raw[:], in_=q[0, w, h].rearrange("(i p) d -> p i d", p=P))
             k_raw = qk.tile([P, TILES, HD], BF16, name="k_raw")
-            nc.sync.dma_start(out=k_raw[:], in_=k[0, w, h].rearrange("(i p) d -> p i d", p=P))
+            nc.sync.dma_start(
+                out=k_raw[:].rearrange("p (a e) d -> p a (e d)", e=2),
+                in_=k[0, w, h].rearrange("(a p e) d -> p a (e d)", p=P, e=2),
+            )
             raw[m] = {"q": q_raw, "k": k_raw}
 
         def transpose_qk(m, which):
@@ -119,19 +123,26 @@ def tile_swintransformer_pa_kernel(tc, x, q, k, wv, bv, pos_bias, out):
 
         def turn_bias(u):
             h, i = units[u]
-            source = bias_raw.pop(u)
-            bT_ps = ps_tr.tile([P, TILES, P], BF16, name="bT_ps", tag="tr")
-            for j in range(TILES):
-                nc.tensor.transpose(out=bT_ps[:, j, :], in_=source[:, j * P : (j + 1) * P], identity=ident_bf[:])
+            words = bias_raw.pop(u)[:].bitcast(F32)
+            bT_ps = ps_tr.tile([P, TILES // 2, P], F32, name="bT_ps", tag="tr")
+            for a in range(TILES // 2):
+                nc.tensor.transpose(out=bT_ps[:, a, :], in_=words[:, a * P : (a + 1) * P], identity=ident_f32[:])
 
             def copy_out():
                 if i == 0:
                     biasT[h] = bias_keep.tile([P, TILES, TOK], F32, name="biasT")
-                nc.vector.tensor_scalar(
-                    out=biasT[h][:, :, i * P : (i + 1) * P], in0=bT_ps[:], scalar1=UNSCALE, scalar2=None, op0=ALU.mult
+                bT_words = bias_mid.tile([P, TILES // 2, P], F32, name="bT_words")
+                nc.scalar.copy(out=bT_words[:], in_=bT_ps[:])
+                nc.gpsimd.tensor_scalar(
+                    out=biasT[h][:, :, i * P : (i + 1) * P].rearrange("p (a e) n -> p a e n", e=2),
+                    in0=bT_words[:].bitcast(BF16).rearrange("p a (n e) -> p a e n", e=2),
+                    scalar1=UNSCALE,
+                    scalar2=0.0,
+                    op0=ALU.mult,
+                    op1=ALU.add,
                 )
 
-            later_vector.append(copy_out)
+            later_scalar.append(copy_out)
 
         x_raw = {}
         px = {}
@@ -160,10 +171,11 @@ def tile_swintransformer_pa_kernel(tc, x, q, k, wv, bv, pos_bias, out):
                     )
 
             def copy_out():
-                nc.scalar.copy(
-                    out=grouped[:].bitcast(F32)[:, j : j + 2, :, :],
-                    in_=xT_ps[:].rearrange("p j u k -> p j k u"),
-                )
+                for e in range(2):
+                    nc.scalar.copy(
+                        out=grouped[:].bitcast(F32)[:, j + e, :, :].rearrange("p (b m) u -> p b m u", b=2),
+                        in_=xT_ps[:].rearrange("p b u (m e) -> p e b m u", e=2)[:, e],
+                    )
 
             later_scalar.append(copy_out)
 
@@ -363,7 +375,7 @@ def tile_swintransformer_pa_kernel(tc, x, q, k, wv, bv, pos_bias, out):
 
         unit_at = {}
         for u, (h, i) in enumerate(units):
-            unit_at[i - 3 if h == 0 else (h - 1) * NW * TILES + 7 + 3 * i] = u
+            unit_at[i - 4 if h == 0 else (h - 1) * NW * TILES + 7 + 3 * i] = u
 
         def v_slot(w, s):
             return s - (w * TILES + LAG - (V_SLOTS - 1))

@@ -34,6 +34,7 @@ SCALE = 1.0 / math.sqrt(D)
 UNSCALE = math.sqrt(D)
 MASKED = -1.0e30
 LAG = 6
+RUN_LAG = LAG - QUAD + 1
 HEAD_STEPS = 5
 V_SLOTS = 10
 
@@ -463,8 +464,8 @@ def tile_swintransformer_pa_kernel(tc, x, q, k, wv, bv, pos_bias, out):
             vector_side(s)
             if group_due(s - 1):
                 add_sums((s - 1) // QUAD)
-            if group_due(s - LAG - 1):
-                normalise((s - LAG - 1) // QUAD)
+            if group_due(s - RUN_LAG - 1):
+                normalise((s - RUN_LAG - 1) // QUAD)
             if group_due(s - 2):
                 invert_sums((s - 2) // QUAD)
             if tile_exists(s + 1):
@@ -479,6 +480,7 @@ def tile_swintransformer_pa_kernel(tc, x, q, k, wv, bv, pos_bias, out):
             if tile_exists(s - 1):
                 copy_eT(s - 1)
             transposes_side(s)
-            if tile_exists(s - LAG):
-                multiply_v(s - LAG)
+            if group_due(s - RUN_LAG):
+                for n in range(s - RUN_LAG - QUAD + 1, s - RUN_LAG + 1):
+                    multiply_v(n)
             mx_side(s)

@@ -95,10 +95,10 @@ def tile_swintransformer_pa_kernel(tc, x, q, k, wv, bv, pos_bias, out):
 
             def copy_out():
                 turned_sb = qk.tile([P, TILES, P], BF16, name=which + "T")
-                nc.scalar.copy(out=turned_sb[:], in_=turned_ps[:])
+                nc.vector.tensor_copy(out=turned_sb[:], in_=turned_ps[:])
                 turned[(m, which)] = turned_sb
 
-            later_scalar.append(copy_out)
+            later_vector.append(copy_out)
 
         units = [(h, i) for h in range(HEADS) for i in range(TILES)]
         bias_raw = {}

@@ -55,9 +55,8 @@ def tile_swintransformer_pa_kernel(tc, x, q, k, wv, bv, pos_bias, out):
         work = ctx.enter_context(tc.tile_pool(name="work", bufs=3))
         coded = ctx.enter_context(tc.tile_pool(name="coded", bufs=LAG))
         stat = ctx.enter_context(tc.tile_pool(name="stat", bufs=6))
-        ps_lg = ctx.enter_context(tc.psum_pool(name="ps_lg", bufs=4))
+        ps_lg = ctx.enter_context(tc.psum_pool(name="ps_lg", bufs=5))
         ps_tr = ctx.enter_context(tc.psum_pool(name="ps_tr", bufs=3))
-        ps_o = ctx.enter_context(tc.psum_pool(name="ps_o", bufs=1))
         ctx.enter_context(tc.manual_schedule())
 
         ident_bf = const.tile([P, P], BF16, name="ident_bf")
@@ -346,7 +345,7 @@ def tile_swintransformer_pa_kernel(tc, x, q, k, wv, bv, pos_bias, out):
             v_codes, v_scales = values[w]
             e_codes, e_scales = weights.pop(n)
             if r == 0:
-                o_banks[group] = ps_o.tile([P, QUAD, HD], F32, name="o_ps")
+                o_banks[group] = ps_tr.tile([P, QUAD, HD], F32, name="o_ps", tag="tr")
             cols = slice(h * HD, (h + 1) * HD)
             for g in range(PASSES):
                 queries = slice(g * P, (g + 1) * P)

@@ -64,6 +64,9 @@ def tile_swintransformer_pa_kernel(tc, x, q, k, wv, bv, pos_bias, out):
         ident_f32 = const.tile([P, P], F32, name="ident_f32")
         make_identity(nc, ident_f32[:])
 
+        warm = const.tile([P, 1], F32, name="warm")
+        nc.scalar.activation(out=warm[:], in_=ident_f32[:, 0:1], func=ACT.Exp)
+
         later_scalar = []
         later_vector = []
 
@@ -143,6 +146,21 @@ def tile_swintransformer_pa_kernel(tc, x, q, k, wv, bv, pos_bias, out):
                 )
 
             later_scalar.append(copy_out)
+
+        w_raw = const.tile([P, PACK, D], BF16, name="w_raw")
+        w_grouped = const.tile([P, D, PACK], BF16, name="w_grouped", align_bytes=64)
+        w_codes = const.tile([P, D], U32, name="w_codes", align_bytes=64)
+        w_scales = const.tile([P, D], U8, name="w_scales", align_bytes=64)
+
+        def group_w():
+            nc.vector.tensor_copy(out=w_grouped[:], in_=w_raw[:].rearrange("p t n -> p n t"))
+
+        def quantise_w():
+            nc.vector.quantize_mx(
+                out=w_codes[:].bitcast(FP8X4),
+                scales=w_scales[:],
+                in_=w_grouped[:].rearrange("p n t -> p (n t)"),
+            )
 
         x_raw = {}
         px = {}
@@ -373,9 +391,14 @@ def tile_swintransformer_pa_kernel(tc, x, q, k, wv, bv, pos_bias, out):
                 in_=o_sb[:],
             )
 
+        quiet = [
+            t
+            for t in range(TILES, NW * TILES)
+            if (t - RUN_LAG) % QUAD != QUAD - 1 and (t + HEAD_STEPS) % TILES not in (0, 1)
+        ]
         unit_at = {}
         for u, (h, i) in enumerate(units):
-            unit_at[i - 4 if h == 0 else (h - 1) * NW * TILES + 7 + 3 * i] = u
+            unit_at[i - 4 if h == 0 else (h - 1) * NW * TILES + quiet[i]] = u
 
         def v_slot(w, s):
             return s - (w * TILES + LAG - (V_SLOTS - 1))
@@ -383,6 +406,10 @@ def tile_swintransformer_pa_kernel(tc, x, q, k, wv, bv, pos_bias, out):
         def vector_side(s):
             for w in range(NW):
                 slot = v_slot(w, s)
+                if w == 0 and slot == 0:
+                    group_w()
+                if w == 0 and slot == 1:
+                    quantise_w()
                 if slot in (2, 3):
                     quantise_x(w, slot - 2)
                 if slot in (7, 9):
@@ -422,14 +449,13 @@ def tile_swintransformer_pa_kernel(tc, x, q, k, wv, bv, pos_bias, out):
                 if slot in (5, 7):
                     group_v(w, (slot - 5) // 2)
 
-        load_qk(0)
         load_bias(0)
-        load_x(0)
-        w_raw = const.tile([P, PACK, D], BF16, name="w_raw")
+        load_qk(0)
         nc.sync.dma_start(
             out=w_raw[:].rearrange("p (u e) n -> p u (e n)", e=2),
             in_=wv.rearrange("(u p e) n -> p u (e n)", u=2, e=2),
         )
+        load_x(0)
         bv_sb = const.tile([P, D], BF16, name="bv_sb")
         nc.sync.dma_start(out=bv_sb[:], in_=bv.partition_broadcast(P))
         load_bias(1)
@@ -437,16 +463,6 @@ def tile_swintransformer_pa_kernel(tc, x, q, k, wv, bv, pos_bias, out):
         load_qk(1)
         load_x(1)
         mask_bias(0)
-
-        w_grouped = const.tile([P, D, PACK], BF16, name="w_grouped", align_bytes=64)
-        nc.vector.tensor_copy(out=w_grouped[:], in_=w_raw[:].rearrange("p t n -> p n t"))
-        w_codes = const.tile([P, D], U32, name="w_codes", align_bytes=64)
-        w_scales = const.tile([P, D], U8, name="w_scales", align_bytes=64)
-        nc.vector.quantize_mx(
-            out=w_codes[:].bitcast(FP8X4),
-            scales=w_scales[:],
-            in_=w_grouped[:].rearrange("p n t -> p (n t)"),
-        )
 
         def tile_exists(n):
             return 0 <= n < N_TILES

import math
from contextlib import ExitStack

import concourse.mybir as mybir
from concourse.masks import make_identity

BF16 = mybir.dt.bfloat16
F32 = mybir.dt.float32
U32 = mybir.dt.uint32
U8 = mybir.dt.uint8
FP8X4 = mybir.dt.float8_e4m3fn_x4
ALU = mybir.AluOpType
ACT = mybir.ActivationFunctionType
AXIS = mybir.AxisListType

P = 128
PACK = 4
WIN = 32
GRID = 2
NW = GRID * GRID
HEADS = 4
TOK = WIN * WIN
D = 512
HD = D // HEADS
TILES = TOK // P
PASSES = TOK // (P * PACK)
BANK = 512
HALVES = TOK // BANK
QUAD = BANK // HD
PAIRS = NW * HEADS
N_TILES = PAIRS * TILES
ROWS = 2 * P // WIN
SCALE = 1.0 / math.sqrt(D)
UNSCALE = math.sqrt(D)
MASKED = -1.0e30
LAG = 6
RUN_LAG = LAG - QUAD + 1
HEAD_STEPS = 5
V_SLOTS = 10

FLOPS = 2 * NW * TOK * D * D + 2 * (2 * PAIRS * TOK * TOK * HD)


def tile_swintransformer_pa_kernel(tc, x, q, k, wv, bv, pos_bias, out):
    nc = tc.nc
    with ExitStack() as ctx:
        const = ctx.enter_context(tc.tile_pool(name="const", bufs=1))
        bias_in = ctx.enter_context(tc.tile_pool(name="bias_in", bufs=3))
        bias_mid = ctx.enter_context(tc.tile_pool(name="bias_mid", bufs=2))
        bias_keep = ctx.enter_context(tc.tile_pool(name="bias_keep", bufs=2))
        xin = ctx.enter_context(tc.tile_pool(name="xin", bufs=2))
        proj = ctx.enter_context(tc.tile_pool(name="proj", bufs=1))
        vkeep = ctx.enter_context(tc.tile_pool(name="vkeep", bufs=NW))
        qk = ctx.enter_context(tc.tile_pool(name="qk", bufs=2))
        work = ctx.enter_context(tc.tile_pool(name="work", bufs=3))
        coded = ctx.enter_context(tc.tile_pool(name="coded", bufs=LAG))
        stat = ctx.enter_context(tc.tile_pool(name="stat", bufs=6))
        ps_lg = ctx.enter_context(tc.psum_pool(name="ps_lg", bufs=5))
        ps_tr = ctx.enter_context(tc.psum_pool(name="ps_tr", bufs=3))
        ctx.enter_context(tc.manual_schedule())

        ident_bf = const.tile([P, P], BF16, name="ident_bf")
        make_identity(nc, ident_bf[:])
        ident_f32 = const.tile([P, P], F32, name="ident_f32")
        make_identity(nc, ident_f32[:])

        warm = const.tile([P, 1], F32, name="warm")
        nc.scalar.activation(out=warm[:], in_=ident_f32[:, 0:1], func=ACT.Exp)

        later_scalar = []
        later_vector = []

        def run_all(calls):
            for call in list(calls):
                call()
            calls.clear()

        raw = {}
        turned = {}

        def load_qk(m):
            h, w = divmod(m, NW)
            q_raw = qk.tile([P, TILES, HD], BF16, name="q_raw")
            nc.sync.dma_start(out=q_raw[:], in_=q[0, w, h].rearrange("(i p) d -> p i d", p=P))
            k_raw = qk.tile([P, TILES, HD], BF16, name="k_raw")
            nc.sync.dma_start(
                out=k_raw[:].rearrange("p (a e) d -> p a (e d)", e=2),
                in_=k[0, w, h].rearrange("(a p e) d -> p a (e d)", p=P, e=2),
            )
            raw[m] = {"q": q_raw, "k": k_raw}

        def transpose_qk(m, which):
            source = raw[m].pop(which)
            turned_ps = ps_tr.tile([P, TILES, P], BF16, name="turned_ps", tag="tr")
            for i in range(TILES):
                nc.tensor.transpose(out=turned_ps[:, i, :], in_=source[:, i, :], identity=ident_bf[:])

            def copy_out():
                turned_sb = qk.tile([P, TILES, P], BF16, name=which + "T")
                nc.vector.tensor_copy(out=turned_sb[:], in_=turned_ps[:])
                turned[(m, which)] = turned_sb

            later_vector.append(copy_out)

        units = [(h, i) for h in range(HEADS) for i in range(TILES)]
        bias_raw = {}
        biasT = {}

        def load_bias(u):
            h, i = units[u]
            bias_raw[u] = bias_in.tile([P, TOK], BF16, name="bias_raw")
            nc.sync.dma_start(out=bias_raw[u][:], in_=pos_bias[h, i * P : (i + 1) * P, :])

        def mask_bias(u):
            h, i = units[u]
            block = bias_raw[u][:, i * P : (i + 1) * P]
            nc.gpsimd.affine_select(
                out=block,
                in_=block,
                compare_op=ALU.not_equal,
                fill=MASKED,
                base=0,
                pattern=[[-1, P]],
                channel_multiplier=1,
            )

        def turn_bias(u):
            h, i = units[u]
            words = bias_raw.pop(u)[:].bitcast(F32)
            bT_ps = ps_tr.tile([P, TILES // 2, P], F32, name="bT_ps", tag="tr")
            for a in range(TILES // 2):
                nc.tensor.transpose(out=bT_ps[:, a, :], in_=words[:, a * P : (a + 1) * P], identity=ident_f32[:])

            def copy_out():
                if i == 0:
                    biasT[h] = bias_keep.tile([P, TILES, TOK], F32, name="biasT")
                bT_words = bias_mid.tile([P, TILES // 2, P], F32, name="bT_words")
                nc.scalar.copy(out=bT_words[:], in_=bT_ps[:])
                nc.gpsimd.tensor_scalar(
                    out=biasT[h][:, :, i * P : (i + 1) * P].rearrange("p (a e) n -> p a e n", e=2),
                    in0=bT_words[:].bitcast(BF16).rearrange("p a (n e) -> p a e n", e=2),
                    scalar1=UNSCALE,
                    scalar2=0.0,
                    op0=ALU.mult,
                    op1=ALU.add,
                )

            later_scalar.append(copy_out)

        w_raw = const.tile([P, PACK, D], BF16, name="w_raw")
        w_grouped = const.tile([P, D, PACK], BF16, name="w_grouped", align_bytes=64)
        w_codes = const.tile([P, D], U32, name="w_codes", align_bytes=64)
        w_scales = const.tile([P, D], U8, name="w_scales", align_bytes=64)

        def group_w():
            nc.vector.tensor_copy(out=w_grouped[:], in_=w_raw[:].rearrange("p t n -> p n t"))

        def quantise_w():
            nc.vector.quantize_mx(
                out=w_codes[:].bitcast(FP8X4),
                scales=w_scales[:],
                in_=w_grouped[:].rearrange("p n t -> p (n t)"),
            )

        x_raw = {}
        px = {}
        values = {}

        def load_x(w):
            wi, wj = divmod(w, GRID)
            pixels = x[0, wi * WIN : (wi + 1) * WIN, wj * WIN : (wj + 1) * WIN, :]
            by_row = pixels.rearrange("(a r) (c e) d -> r c a (e d)", r=ROWS, e=2)
            tile_x = xin.tile([P, TILES, D], BF16, name="x_raw")
            slots = tile_x[:].rearrange("p (a e) d -> p a (e d)", e=2)
            for r in range(ROWS):
                nc.sync.dma_start(out=slots[r * (WIN // 2) : (r + 1) * (WIN // 2), :, :], in_=by_row[r])
            x_raw[w] = tile_x

        def turn_x(w, j):
            if j == 0:
                px["grouped"] = proj.tile([P, TILES, P, PACK], BF16, name="x_grouped", align_bytes=64)
            grouped = px["grouped"]
            xT_ps = ps_tr.tile([P, 2, 2, P], F32, name="xT_ps", tag="tr")
            for jj in range(2):
                words = x_raw[w][:, j + jj, :].bitcast(F32)
                for u in range(2):
                    nc.tensor.transpose(
                        out=xT_ps[:, jj, u, :], in_=words[:, u * P : (u + 1) * P], identity=ident_f32[:]
                    )

            def copy_out():
                for e in range(2):
                    nc.scalar.copy(
                        out=grouped[:].bitcast(F32)[:, j + e, :, :].rearrange("p (b m) u -> p b m u", b=2),
                        in_=xT_ps[:].rearrange("p b u (m e) -> p e b m u", e=2)[:, e],
                    )

            later_scalar.append(copy_out)

        def quantise_x(w, g):
            if g == 0:
                px["codes"] = proj.tile([P, TOK], U32, name="x_codes", align_bytes=64)
                px["scales"] = proj.tile([P, TOK], U8, name="x_scales", align_bytes=64)
            tokens = slice(g * BANK, (g + 1) * BANK)
            nc.vector.quantize_mx(
                out=px["codes"][:, tokens].bitcast(FP8X4),
                scales=px["scales"][:, tokens],
                in_=px["grouped"][:, g * PACK : (g + 1) * PACK, :, :].rearrange("p j k t -> p (j k t)"),
            )

        def project(w, j):
            if j == 0:
                px["v_bf"] = proj.tile([P, TILES, D], BF16, name="v_bf")
            v_bf = px["v_bf"]
            v_ps = ps_tr.tile([P, D], F32, name="v_ps", tag="tr")
            tokens = slice(j * P, (j + 1) * P)
            nc.tensor.matmul_mx(
                out=v_ps[:],
                lhsT=px["codes"][:, tokens].bitcast(FP8X4),
                lhsT_scale=px["scales"][:, tokens],
                rhs=w_codes[:].bitcast(FP8X4),
                rhs_scale=w_scales[:],
                start=True,
                stop=True,
            )

            def add_bv():
                nc.vector.tensor_tensor(out=v_bf[:, j, :], in0=v_ps[:], in1=bv_sb[:], op=ALU.add)

            later_vector.append(add_bv)

        def group_v(w, g):
            if g == 0:
                px["v_grouped"] = proj.tile([P, PASSES, D, PACK], BF16, name="v_grouped", align_bytes=64)
            for half in range(2):
                cols = slice(half * D // 2, (half + 1) * D // 2)
                nc.gpsimd.tensor_scalar(
                    out=px["v_grouped"][:, g, cols, :],
                    in0=px["v_bf"][:, g * PACK : (g + 1) * PACK, cols].rearrange("p t c -> p c t"),
                    scalar1=1.0,
                    scalar2=0.0,
                    op0=ALU.mult,
                    op1=ALU.add,
                )

        def quantise_v(w, g):
            if g == 0:
                v_codes = vkeep.tile([P, PASSES, D], U32, name="v_codes", align_bytes=64)
                v_scales = vkeep.tile([P, PASSES, D], U8, name="v_scales", align_bytes=64)
                values[w] = (v_codes, v_scales)
            v_codes, v_scales = values[w]
            nc.vector.quantize_mx(
                out=v_codes[:, g, :].bitcast(FP8X4),
                scales=v_scales[:, g, :],
                in_=px["v_grouped"][:, g, :, :].rearrange("p c t -> p (c t)"),
            )

        lg_banks = {}
        neg_max = {}
        sums = {}
        recips = {}
        e_rows = {}
        eT_banks = {}
        e_groups = {}
        weights = {}
        o_banks = {}

        def place(n):
            m, i = divmod(n, TILES)
            h, w = divmod(m, NW)
            return m, h, w, i

        def fill_logits(n):
            m, h, w, i = place(n)
            qT, kT = turned[(m, "q")], turned[(m, "k")]
            lg_banks[n] = []
            for c in range(HALVES):
                lg_ps = ps_lg.tile([P, BANK], F32, name="lg_ps", tag="lg")
                nc.tensor.matmul(
                    out=lg_ps[:],
                    lhsT=qT[:, i, :],
                    rhs=kT[:].rearrange("d j p -> d (j p)")[:, c * BANK : (c + 1) * BANK],
                    start=True,
                    stop=False,
                )
                lg_banks[n].append(lg_ps)
            for c in range(HALVES):
                for jj in range(QUAD):
                    nc.tensor.matmul(
                        out=lg_banks[n][c][:, jj * P : (jj + 1) * P],
                        lhsT=biasT[h][:, c * QUAD + jj, i * P : (i + 1) * P],
                        rhs=ident_f32[:],
                        is_transpose=True,
                        start=False,
                        stop=(jj == QUAD - 1),
                    )

        def take_max(n, c):
            unused = work.tile([P, BANK], BF16, name="unused")
            lowest = stat.tile([P, 1], F32, name="lowest%d" % c)
            nc.vector.tensor_scalar(
                out=unused[:],
                in0=lg_banks[n][c][:],
                scalar1=-SCALE,
                scalar2=(None if c == 0 else neg_max[n][:]),
                op0=ALU.mult,
                op1=ALU.min,
                accum_out=lowest[:],
            )
            neg_max[n] = lowest

        def exponentiate(n):
            group, r = divmod(n, QUAD)
            if r == 0:
                sums[group] = stat.tile([P, QUAD, HALVES], F32, name="rowsum")
            e_rows[n] = work.tile([P, TOK], BF16, name="e")
            shift = neg_max.pop(n)
            for c, lg_ps in enumerate(lg_banks.pop(n)):
                nc.scalar.activation(
                    out=e_rows[n][:, c * BANK : (c + 1) * BANK],
                    in_=lg_ps[:],
                    func=ACT.Exp,
                    bias=shift[:],
                    scale=SCALE,
                    accum_out=sums[group][:, r, c : c + 1],
                )

        def add_sums(group):
            total = stat.tile([P, QUAD], F32, name="total")
            nc.vector.tensor_reduce(out=total[:], in_=sums.pop(group)[:], axis=AXIS.X, op=ALU.add)
            sums[group] = total

        def invert_sums(group):
            recips[group] = stat.tile([P, QUAD], F32, name="recip")
            nc.vector.reciprocal(out=recips[group][:], in_=sums.pop(group)[:])

        def turn_e(n):
            words = e_rows.pop(n)[:].bitcast(F32)
            eT_banks[n] = ps_tr.tile([P, TILES // 2, P], F32, name="eT_ps", tag="tr")
            for a in range(TILES // 2):
                nc.tensor.transpose(out=eT_banks[n][:, a, :], in_=words[:, a * P : (a + 1) * P], identity=ident_f32[:])

        def copy_eT(n):
            e_groups[n] = work.tile([P, PASSES, P, PACK], BF16, name="e_grouped", align_bytes=64)
            nc.scalar.copy(
                out=e_groups[n][:].bitcast(F32),
                in_=eT_banks.pop(n)[:].rearrange("p (g u) n -> p g n u", u=2),
            )

        def quantise_e(n):
            e_codes = coded.tile([P, PASSES * P], U32, name="e_codes", align_bytes=64)
            e_scales = coded.tile([P, PASSES * P], U8, name="e_scales", align_bytes=64)
            nc.vector.quantize_mx(
                out=e_codes[:].bitcast(FP8X4),
                scales=e_scales[:],
                in_=e_groups.pop(n)[:].rearrange("p g n t -> p (g n t)"),
            )
            weights[n] = (e_codes, e_scales)

        def multiply_v(n):
            m, h, w, i = place(n)
            group, r = divmod(n, QUAD)
            v_codes, v_scales = values[w]
            e_codes, e_scales = weights.pop(n)
            if r == 0:
                o_banks[group] = ps_tr.tile([P, QUAD, HD], F32, name="o_ps", tag="tr")
            cols = slice(h * HD, (h + 1) * HD)
            for g in range(PASSES):
                queries = slice(g * P, (g + 1) * P)
                nc.tensor.matmul_mx(
                    out=o_banks[group][:, r, :],
                    lhsT=e_codes[:, queries].bitcast(FP8X4),
                    lhsT_scale=e_scales[:, queries],
                    rhs=v_codes[:, g, cols].bitcast(FP8X4),
                    rhs_scale=v_scales[:, g, cols],
                    start=(g == 0),
                    stop=(g == PASSES - 1),
                )

        def normalise(group):
            m, h, w, i = place(group * QUAD)
            o_sb = work.tile([P, QUAD, HD], F32, name="o_sb")
            nc.vector.tensor_tensor(
                out=o_sb[:],
                in0=o_banks.pop(group)[:],
                in1=recips.pop(group)[:].unsqueeze(2).to_broadcast([P, QUAD, HD]),
                op=ALU.mult,
            )
            nc.sync.dma_start(
                out=out[0, w].rearrange("(i p) c -> p i c", p=P)[:, i : i + QUAD, h * HD : (h + 1) * HD],
                in_=o_sb[:],
            )

        quiet = [
            t
            for t in range(TILES, NW * TILES)
            if (t - RUN_LAG) % QUAD != QUAD - 1 and (t + HEAD_STEPS) % TILES not in (0, 1)
        ]
        unit_at = {}
        for u, (h, i) in enumerate(units):
            unit_at[i - 4 if h == 0 else (h - 1) * NW * TILES + quiet[i]] = u

        def v_slot(w, s):
            return s - (w * TILES + LAG - (V_SLOTS - 1))

        def vector_side(s):
            for w in range(NW):
                slot = v_slot(w, s)
                if w == 0 and slot == 0:
                    group_w()
                if w == 0 and slot == 1:
                    quantise_w()
                if slot in (2, 3):
                    quantise_x(w, slot - 2)
                if slot in (7, 9):
                    quantise_v(w, (slot - 7) // 2)

        def transposes_side(s):
            m, i = divmod(s + HEAD_STEPS, TILES)
            if m < PAIRS and i == 0:
                transpose_qk(m, "q")
            if m < PAIRS and i == 1:
                transpose_qk(m, "k")
                if m + 2 < PAIRS:
                    load_qk(m + 2)
            if s in unit_at:
                u = unit_at[s]
                turn_bias(u)
                if u + 1 < len(units):
                    mask_bias(u + 1)
                if u + 3 < len(units):
                    load_bias(u + 3)
            for w in range(NW):
                slot = v_slot(w, s)
                if slot in (0, 1):
                    turn_x(w, 4 * slot)
                    turn_x(w, 4 * slot + 2)
                if slot == 2:
                    x_raw.pop(w)
                    if w + 2 < NW:
                        load_x(w + 2)

        def mx_side(s):
            for w in range(NW):
                slot = v_slot(w, s)
                if 2 <= slot <= 5:
                    project(w, 2 * (slot - 2))
                    project(w, 2 * (slot - 2) + 1)
                if slot in (5, 7):
                    group_v(w, (slot - 5) // 2)

        load_bias(0)
        load_qk(0)
        nc.sync.dma_start(
            out=w_raw[:].rearrange("p (u e) n -> p u (e n)", e=2),
            in_=wv.rearrange("(u p e) n -> p u (e n)", u=2, e=2),
        )
        load_x(0)
        bv_sb = const.tile([P, D], BF16, name="bv_sb")
        nc.sync.dma_start(out=bv_sb[:], in_=bv.partition_broadcast(P))
        load_bias(1)
        load_bias(2)
        load_qk(1)
        load_x(1)
        mask_bias(0)

        def tile_exists(n):
            return 0 <= n < N_TILES

        def group_due(n):
            return tile_exists(n) and n % QUAD == QUAD - 1

        for s in range(-HEAD_STEPS, N_TILES + LAG + 1):
            if tile_exists(s + 1):
                fill_logits(s + 1)
            if tile_exists(s):
                exponentiate(s)
            run_all(later_vector)
            vector_side(s)
            if group_due(s - 1):
                add_sums((s - 1) // QUAD)
            if group_due(s - RUN_LAG - 1):
                normalise((s - RUN_LAG - 1) // QUAD)
            if group_due(s - 2):
                invert_sums((s - 2) // QUAD)
            if tile_exists(s + 1):
                take_max(s + 1, 0)
            if tile_exists(s - 2):
                quantise_e(s - 2)
            if tile_exists(s + 1):
                take_max(s + 1, 1)
            if tile_exists(s - 1):
                turn_e(s - 1)
            run_all(later_scalar)
            if tile_exists(s - 1):
                copy_eT(s - 1)
            transposes_side(s)
            if group_due(s - RUN_LAG):
                for n in range(s - RUN_LAG - QUAD + 1, s - RUN_LAG + 1):
                    multiply_v(n)
            mx_side(s)
